import numpy as np
import ml_dtypes

BF16 = ml_dtypes.bfloat16


def bf(x):
    return np.asarray(x, np.float32).astype(BF16)


def f32(x):
    return np.asarray(x, np.float32)


def f64(x):
    return np.asarray(x).astype(np.float64)


def striped(idx):
    return np.tile(idx.reshape(-1, 16).T, (8, 1))


C, S, NN, B, N = 256, 4096, 17, 128, 2176
LN_EPS = 1e-5
LEAKY_SLOPE = 0.01


def setup_inputs():
    lim = 1.0 / np.sqrt(C)
    return {
        "x": f32(np.random.standard_normal((C, S))),
        "w_l": bf(np.random.uniform(-lim, lim, (C, C))),
        "w_r": bf(np.random.uniform(-lim, lim, (C, C))),
        "b_l": f32(0.1 * np.random.standard_normal((C, 1))),
        "gamma": f32(1.0 + 0.1 * np.random.standard_normal((C, 1))),
        "beta": f32(0.1 * np.random.standard_normal((C, 1))),
        "offs": striped(np.random.permutation(np.tile(np.arange(S), 2))[:N]),
    }


def reference(x, w_l, w_r, b_l, gamma, beta, offs):
    idx = offs[:16].T.reshape(-1)
    h = f64(x)[:, idx]
    hn = h.reshape(C, NN, B)
    m = ((hn.sum(axis=1, keepdims=True) - hn) / (NN - 1)).reshape(C, N)
    z = f64(w_l).T @ m + f64(b_l) + f64(w_r).T @ h
    mu = z.mean(axis=0, keepdims=True)
    var = np.square(z - mu).mean(axis=0, keepdims=True)
    y = (z - mu) / np.sqrt(var + LN_EPS) * f64(gamma) + f64(beta)
    return np.maximum(y, LEAKY_SLOPE * y) + h

@@ -1,0 +1,127 @@
+import concourse.mybir as mybir
+
+F32 = mybir.dt.float32
+BF16 = mybir.dt.bfloat16
+U16 = mybir.dt.uint16
+ALU = mybir.AluOpType
+ACT = mybir.ActivationFunctionType
+AXIS_X = mybir.AxisListType.X
+
+P = 128
+C = 256
+CB = C // P
+S = 4096
+NODES = 17
+NICHES = 128
+N = NODES * NICHES
+CHUNK = 512
+LN_EPS = 1e-5
+LEAKY_SLOPE = 0.01
+
+FLOPS = 2 * 2 * C * C * N
+
+
+def tile_gnnnicheencoder_kernel(tc, x, w_l, w_r, b_l, gamma, beta, offs, out):
+    nc = tc.nc
+    with (
+        tc.tile_pool(name="held", bufs=1) as held,
+        tc.tile_pool(name="work", bufs=3) as work,
+        tc.psum_pool(name="psum", bufs=1) as psum,
+    ):
+        offsets = held.tile([P, N // 16], U16, name="offsets")
+        nc.sync.dma_start(offsets[:], offs)
+
+        store = [held.tile([P, S], F32, name=f"store{cb}") for cb in range(CB)]
+        for cb in range(CB):
+            rows = x[cb * P : (cb + 1) * P, :]
+            nc.sync.dma_start(store[cb][:, : S // 2], rows[:, : S // 2])
+            nc.scalar.dma_start(store[cb][:, S // 2 :], rows[:, S // 2 :])
+
+        wl_raw = held.tile([P, CB, C], BF16, name="wl_raw")
+        wr_raw = held.tile([P, CB, C], BF16, name="wr_raw")
+        nc.gpsimd.dma_start(wl_raw[:], w_l.rearrange("(kb p) c -> p kb c", p=P))
+        nc.gpsimd.dma_start(wr_raw[:], w_r.rearrange("(kb p) c -> p kb c", p=P))
+
+        bias_col = held.tile([P, CB], F32, name="bias_col")
+        gamma_col = held.tile([P, CB], F32, name="gamma_col")
+        beta_col = held.tile([P, CB], F32, name="beta_col")
+        with nc.allow_non_contiguous_dma(reason="256 floats, one to a partition and block"):
+            for col, vec in ((bias_col, b_l), (gamma_col, gamma), (beta_col, beta)):
+                nc.gpsimd.dma_start(col[:], vec.rearrange("(cb p) o -> p (cb o)", p=P))
+        bias_all = held.tile([P, C], F32, name="bias_all")
+        nc.gpsimd.dma_start(bias_all[:], b_l.rearrange("c o -> (c o)").partition_broadcast(P))
+
+        wl_c = held.tile([P, CB, C], BF16, name="wl_c")
+        wr_c = held.tile([P, CB, C], BF16, name="wr_c")
+        for raw, centred, tag in ((wl_raw, wl_c, "l"), (wr_raw, wr_c, "r")):
+            neg_mean = held.tile([P, CB], F32, name=f"neg_mean_{tag}")
+            nc.vector.tensor_reduce(neg_mean[:], raw[:], axis=AXIS_X, op=ALU.add)
+            nc.vector.tensor_scalar_mul(neg_mean[:], neg_mean[:], -1.0 / C)
+            for kb in range(CB):
+                nc.vector.tensor_scalar_add(centred[:, kb, :], raw[:, kb, :], neg_mean[:, kb : kb + 1])
+        neg_bias_mean = held.tile([P, 1], F32, name="neg_bias_mean")
+        nc.vector.tensor_reduce(neg_bias_mean[:], bias_all[:], axis=AXIS_X, op=ALU.add)
+        nc.vector.tensor_scalar_mul(neg_bias_mean[:], neg_bias_mean[:], -1.0 / C)
+        bias_c = held.tile([P, CB], F32, name="bias_c")
+        nc.vector.tensor_scalar_add(bias_c[:], bias_col[:], neg_bias_mean[:, 0:1])
+
+        mean_mat = held.tile([P, P], BF16, name="mean_mat")
+        nc.vector.memset(mean_mat[:], 1.0 / C)
+        eps = held.tile([P, 1], F32, name="eps")
+        nc.vector.memset(eps[:], LN_EPS)
+
+        h = [held.tile([P, N], F32, name=f"h{cb}") for cb in range(CB)]
+        h_bf = [held.tile([P, N], BF16, name=f"h_bf{cb}") for cb in range(CB)]
+        m_bf = [held.tile([P, N], BF16, name=f"m_bf{cb}") for cb in range(CB)]
+        for cb in range(CB):
+            nc.scalar.activation(h[cb][:], store[cb][:].indirect(offsets[:]), ACT.Copy)
+            nc.vector.tensor_copy(h_bf[cb][:], h[cb][:])
+            sum16 = held.tile([P, NICHES], F32, name=f"sum16_{cb}")
+            nc.vector.tensor_reduce(
+                sum16[:], h[cb][:].rearrange("p (n q) -> p q n", q=NICHES), axis=AXIS_X, op=ALU.add
+            )
+            nc.vector.tensor_scalar_mul(sum16[:], sum16[:], 1.0 / (NODES - 1))
+            nc.vector.scalar_tensor_tensor(
+                m_bf[cb][:].rearrange("p (n q) -> p n q", q=NICHES),
+                h[cb][:].rearrange("p (n q) -> p n q", q=NICHES),
+                -1.0 / (NODES - 1),
+                sum16[:].unsqueeze(1).to_broadcast([P, NODES, NICHES]),
+                op0=ALU.mult,
+                op1=ALU.add,
+            )
+
+        for lo in range(0, N, CHUNK):
+            width = min(CHUNK, N - lo)
+            cols = slice(lo, lo + width)
+            zc = []
+            squares = []
+            for cb in range(CB):
+                outs = slice(cb * P, (cb + 1) * P)
+                bank = psum.tile([P, width], F32, name=f"zc{cb}", bufs=2)
+                nc.tensor.matmul(bank[:], wr_c[:, 0, outs], h_bf[0][:, cols], start=True, stop=False)
+                nc.tensor.matmul(bank[:], wr_c[:, 1, outs], h_bf[1][:, cols], start=False, stop=False)
+                nc.tensor.matmul(bank[:], wl_c[:, 0, outs], m_bf[0][:, cols], start=False, stop=False)
+                nc.tensor.matmul(bank[:], wl_c[:, 1, outs], m_bf[1][:, cols], start=False, stop=True)
+                zc.append(bank)
+                sq = work.tile([P, width], BF16, name=f"sq{cb}")
+                nc.scalar.activation(sq[:], bank[:], ACT.Square, bias=bias_c[:, cb : cb + 1])
+                squares.append(sq)
+            var = psum.tile([P, width], F32, name="var", bufs=2)
+            nc.tensor.matmul(var[:], mean_mat[:], squares[0][:], start=True, stop=False)
+            nc.tensor.matmul(var[:], mean_mat[:], squares[1][:], start=False, stop=True)
+            rstd = work.tile([P, width], F32, name="rstd")
+            nc.scalar.activation(rstd[:], var[:], ACT.Abs_reciprocal_sqrt, bias=eps[:, 0:1])
+            for cb in range(CB):
+                normed = work.tile([P, width], F32, name="normed")
+                nc.vector.scalar_tensor_tensor(
+                    normed[:], zc[cb][:], bias_c[:, cb : cb + 1], rstd[:], op0=ALU.add, op1=ALU.mult
+                )
+                y = work.tile([P, width], F32, name="y")
+                nc.scalar.activation(
+                    y[:], normed[:], ACT.Identity, bias=beta_col[:, cb : cb + 1], scale=gamma_col[:, cb : cb + 1]
+                )
+                leaky = work.tile([P, width], F32, name="leaky")
+                nc.vector.scalar_tensor_tensor(leaky[:], y[:], LEAKY_SLOPE, y[:], op0=ALU.mult, op1=ALU.max)
+                result = work.tile([P, width], F32, name="result")
+                nc.vector.tensor_add(result[:], leaky[:], h[cb][:, cols])
+                nc.sync.dma_start(out[cb * P : (cb + 1) * P, cols], result[:])

@@ -1,4 +1,5 @@
 import concourse.mybir as mybir
+from concourse.masks import make_identity
 
 F32 = mybir.dt.float32
 BF16 = mybir.dt.bfloat16
@@ -14,114 +15,191 @@ S = 4096
 NODES = 17
 NICHES = 128
 N = NODES * NICHES
-CHUNK = 512
 LN_EPS = 1e-5
 LEAKY_SLOPE = 0.01
 
 FLOPS = 2 * 2 * C * C * N
 
+PIECE_NODES = (5, 4, 4, 4)
+CHUNK_NODES = (2, 4, 4, 4, 3)
+CHUNKS_AHEAD = 3
+
+
+def spans(node_counts):
+    ranges = []
+    first = 0
+    for nodes in node_counts:
+        ranges.append((first * NICHES, (first + nodes) * NICHES))
+        first += nodes
+    return ranges
+
+
+def by_node(ap):
+    return ap.rearrange("p (n q) -> p n q", q=NICHES)
+
 
 def tile_gnnnicheencoder_kernel(tc, x, w_l, w_r, b_l, gamma, beta, offs, out):
     nc = tc.nc
+    pieces = spans(PIECE_NODES)
+    chunks = spans(CHUNK_NODES)
+    n_pieces = len(pieces)
+    n_chunks = len(chunks)
     with (
         tc.tile_pool(name="held", bufs=1) as held,
-        tc.tile_pool(name="work", bufs=3) as work,
+        tc.tile_pool(name="work", bufs=4) as work,
         tc.psum_pool(name="psum", bufs=1) as psum,
     ):
         offsets = held.tile([P, N // 16], U16, name="offsets")
         nc.sync.dma_start(offsets[:], offs)
 
-        store = [held.tile([P, S], F32, name=f"store{cb}") for cb in range(CB)]
-        for cb in range(CB):
-            rows = x[cb * P : (cb + 1) * P, :]
-            nc.sync.dma_start(store[cb][:, : S // 2], rows[:, : S // 2])
-            nc.scalar.dma_start(store[cb][:, S // 2 :], rows[:, S // 2 :])
-
+        vectors = (b_l, gamma, beta)
+        rows = held.tile([P, C], F32, name="rows")
+        nc.vector.memset(rows[:], 0.0)
+        for r, vec in enumerate(vectors):
+            nc.sync.dma_start(rows[r : r + 1, :], vec.rearrange("c o -> o c"))
         wl_raw = held.tile([P, CB, C], BF16, name="wl_raw")
         wr_raw = held.tile([P, CB, C], BF16, name="wr_raw")
-        nc.gpsimd.dma_start(wl_raw[:], w_l.rearrange("(kb p) c -> p kb c", p=P))
-        nc.gpsimd.dma_start(wr_raw[:], w_r.rearrange("(kb p) c -> p kb c", p=P))
-
-        bias_col = held.tile([P, CB], F32, name="bias_col")
-        gamma_col = held.tile([P, CB], F32, name="gamma_col")
-        beta_col = held.tile([P, CB], F32, name="beta_col")
-        with nc.allow_non_contiguous_dma(reason="256 floats, one to a partition and block"):
-            for col, vec in ((bias_col, b_l), (gamma_col, gamma), (beta_col, beta)):
-                nc.gpsimd.dma_start(col[:], vec.rearrange("(cb p) o -> p (cb o)", p=P))
-        bias_all = held.tile([P, C], F32, name="bias_all")
-        nc.gpsimd.dma_start(bias_all[:], b_l.rearrange("c o -> (c o)").partition_broadcast(P))
-
-        wl_c = held.tile([P, CB, C], BF16, name="wl_c")
-        wr_c = held.tile([P, CB, C], BF16, name="wr_c")
-        for raw, centred, tag in ((wl_raw, wl_c, "l"), (wr_raw, wr_c, "r")):
-            neg_mean = held.tile([P, CB], F32, name=f"neg_mean_{tag}")
-            nc.vector.tensor_reduce(neg_mean[:], raw[:], axis=AXIS_X, op=ALU.add)
-            nc.vector.tensor_scalar_mul(neg_mean[:], neg_mean[:], -1.0 / C)
-            for kb in range(CB):
-                nc.vector.tensor_scalar_add(centred[:, kb, :], raw[:, kb, :], neg_mean[:, kb : kb + 1])
-        neg_bias_mean = held.tile([P, 1], F32, name="neg_bias_mean")
-        nc.vector.tensor_reduce(neg_bias_mean[:], bias_all[:], axis=AXIS_X, op=ALU.add)
-        nc.vector.tensor_scalar_mul(neg_bias_mean[:], neg_bias_mean[:], -1.0 / C)
-        bias_c = held.tile([P, CB], F32, name="bias_c")
-        nc.vector.tensor_scalar_add(bias_c[:], bias_col[:], neg_bias_mean[:, 0:1])
+        nc.sync.dma_start(wl_raw[:], w_l.rearrange("(kb p) c -> p kb c", p=P))
+        nc.scalar.dma_start(wr_raw[:], w_r.rearrange("(kb p) c -> p kb c", p=P))
+        store = [held.tile([P, S], F32, name=f"store{cb}") for cb in range(CB)]
+        for cb in range(CB):
+            nc.sync.dma_start(store[cb][:, : S // 2], x[cb * P : (cb + 1) * P, : S // 2])
+            nc.scalar.dma_start(store[cb][:, S // 2 :], x[cb * P : (cb + 1) * P, S // 2 :])
 
         mean_mat = held.tile([P, P], BF16, name="mean_mat")
         nc.vector.memset(mean_mat[:], 1.0 / C)
         eps = held.tile([P, 1], F32, name="eps")
         nc.vector.memset(eps[:], LN_EPS)
+        identity = held.tile([P, P], F32, name="identity")
+        make_identity(nc, identity[:])
+        warm = held.tile([P, 1], F32, name="warm")
+        nc.scalar.activation(warm[:], eps[:], ACT.Abs_reciprocal_sqrt)
 
-        h = [held.tile([P, N], F32, name=f"h{cb}") for cb in range(CB)]
-        h_bf = [held.tile([P, N], BF16, name=f"h_bf{cb}") for cb in range(CB)]
-        m_bf = [held.tile([P, N], BF16, name=f"m_bf{cb}") for cb in range(CB)]
+        neg_bias_mean = held.tile([1, 1], F32, name="neg_bias_mean")
+        nc.vector.tensor_reduce(neg_bias_mean[:], rows[0:1, :], axis=AXIS_X, op=ALU.add)
+        nc.vector.tensor_scalar_mul(neg_bias_mean[:], neg_bias_mean[:], -1.0 / C)
+        nc.vector.tensor_scalar_add(rows[0:1, :], rows[0:1, :], neg_bias_mean[:])
+        turned = psum.tile([P, CB, P], F32, name="turned", tag="var", bufs=2)
         for cb in range(CB):
-            nc.scalar.activation(h[cb][:], store[cb][:].indirect(offsets[:]), ACT.Copy)
-            nc.vector.tensor_copy(h_bf[cb][:], h[cb][:])
-            sum16 = held.tile([P, NICHES], F32, name=f"sum16_{cb}")
-            nc.vector.tensor_reduce(
-                sum16[:], h[cb][:].rearrange("p (n q) -> p q n", q=NICHES), axis=AXIS_X, op=ALU.add
-            )
-            nc.vector.tensor_scalar_mul(sum16[:], sum16[:], 1.0 / (NODES - 1))
-            nc.vector.scalar_tensor_tensor(
-                m_bf[cb][:].rearrange("p (n q) -> p n q", q=NICHES),
-                h[cb][:].rearrange("p (n q) -> p n q", q=NICHES),
-                -1.0 / (NODES - 1),
-                sum16[:].unsqueeze(1).to_broadcast([P, NODES, NICHES]),
-                op0=ALU.mult,
-                op1=ALU.add,
+            nc.tensor.transpose(turned[:, cb, :], rows[:, cb * P : (cb + 1) * P], identity[:])
+        columns = held.tile([P, CB, len(vectors)], F32, name="columns")
+        nc.vector.tensor_copy(columns[:], turned[:, :, 0 : len(vectors)])
+        bias_c = [columns[:, cb, 0:1] for cb in range(CB)]
+        gamma_col = [columns[:, cb, 1:2] for cb in range(CB)]
+        beta_col = [columns[:, cb, 2:3] for cb in range(CB)]
+
+        wl_c = held.tile([P, CB, C], BF16, name="wl_c")
+        wr_c = held.tile([P, CB, C], BF16, name="wr_c")
+        for raw, centred, factor, side in ((wl_raw, wl_c, 1.0 / (NODES - 1), "l"), (wr_raw, wr_c, 1.0, "r")):
+            neg_mean = held.tile([P, CB], F32, name=f"neg_mean_{side}")
+            nc.vector.tensor_reduce(neg_mean[:], raw[:], axis=AXIS_X, op=ALU.add)
+            nc.vector.tensor_scalar_mul(neg_mean[:], neg_mean[:], -1.0 / C)
+            for kb in range(CB):
+                nc.vector.tensor_scalar(
+                    centred[:, kb, :], raw[:, kb, :], neg_mean[:, kb : kb + 1], factor, op0=ALU.add, op1=ALU.mult
+                )
+
+        h = held.tile([P, CB, N], F32, name="h")
+        h_bf = held.tile([P, CB, N], BF16, name="h_bf")
+        m_bf = held.tile([P, CB, N], BF16, name="m_bf")
+        node_sum = held.tile([P, CB, NICHES], F32, name="node_sum")
+
+        def look_up(cb, i):
+            lo, hi = pieces[i]
+            nc.scalar.activation(h[:, cb, lo:hi], store[cb][:].indirect(offsets[:, lo // 16 : hi // 16]), ACT.Copy)
+            nc.gpsimd.tensor_copy(h_bf[:, cb, lo:hi], h[:, cb, lo:hi])
+            in_piece = h[:, cb, lo:hi].rearrange("p (n q) -> p q n", q=NICHES)
+            if i == 0:
+                nc.vector.tensor_reduce(node_sum[:, cb, :], in_piece, axis=AXIS_X, op=ALU.add)
+            else:
+                part = work.tile([P, NICHES], F32, name="part")
+                nc.vector.tensor_reduce(part[:], in_piece, axis=AXIS_X, op=ALU.add)
+                nc.vector.tensor_add(node_sum[:, cb, :], node_sum[:, cb, :], part[:])
+
+        def sum_of_others(cb, k):
+            lo, hi = chunks[k]
+            nc.vector.tensor_sub(
+                by_node(m_bf[:, cb, lo:hi]),
+                node_sum[:, cb, :].unsqueeze(1).to_broadcast([P, CHUNK_NODES[k], NICHES]),
+                by_node(h[:, cb, lo:hi]),
             )
 
-        for lo in range(0, N, CHUNK):
-            width = min(CHUNK, N - lo)
-            cols = slice(lo, lo + width)
-            zc = []
-            squares = []
+        banks = {}
+        rstds = {}
+        ys = {}
+
+        def project(k, weights, operand, kb):
+            lo, hi = chunks[k]
+            opens = weights is wr_c and kb == 0
+            closes = weights is wl_c and kb == CB - 1
             for cb in range(CB):
-                outs = slice(cb * P, (cb + 1) * P)
-                bank = psum.tile([P, width], F32, name=f"zc{cb}", bufs=2)
-                nc.tensor.matmul(bank[:], wr_c[:, 0, outs], h_bf[0][:, cols], start=True, stop=False)
-                nc.tensor.matmul(bank[:], wr_c[:, 1, outs], h_bf[1][:, cols], start=False, stop=False)
-                nc.tensor.matmul(bank[:], wl_c[:, 0, outs], m_bf[0][:, cols], start=False, stop=False)
-                nc.tensor.matmul(bank[:], wl_c[:, 1, outs], m_bf[1][:, cols], start=False, stop=True)
-                zc.append(bank)
-                sq = work.tile([P, width], BF16, name=f"sq{cb}")
-                nc.scalar.activation(sq[:], bank[:], ACT.Square, bias=bias_c[:, cb : cb + 1])
-                squares.append(sq)
-            var = psum.tile([P, width], F32, name="var", bufs=2)
-            nc.tensor.matmul(var[:], mean_mat[:], squares[0][:], start=True, stop=False)
-            nc.tensor.matmul(var[:], mean_mat[:], squares[1][:], start=False, stop=True)
-            rstd = work.tile([P, width], F32, name="rstd")
-            nc.scalar.activation(rstd[:], var[:], ACT.Abs_reciprocal_sqrt, bias=eps[:, 0:1])
+                if opens:
+                    banks[k, cb] = psum.tile([P, hi - lo], F32, name=f"zc{cb}", bufs=CHUNKS_AHEAD)
+                nc.tensor.matmul(
+                    banks[k, cb][:],
+                    weights[:, kb, cb * P : (cb + 1) * P],
+                    operand[:, kb, lo:hi],
+                    start=opens,
+                    stop=closes,
+                )
+
+        def variance(k):
+            lo, hi = chunks[k]
+            var = psum.tile([P, hi - lo], F32, name="var", bufs=2)
             for cb in range(CB):
-                normed = work.tile([P, width], F32, name="normed")
+                sq = work.tile([P, hi - lo], BF16, name="sq")
+                nc.scalar.activation(sq[:], banks[k, cb][:], ACT.Square, bias=bias_c[cb])
+                nc.tensor.matmul(var[:], mean_mat[:], sq[:], start=(cb == 0), stop=(cb == CB - 1))
+            return var
+
+        def reciprocal_std(k, var):
+            lo, hi = chunks[k]
+            rstds[k] = work.tile([P, hi - lo], F32, name="rstd")
+            nc.scalar.activation(rstds[k][:], var[:], ACT.Abs_reciprocal_sqrt, bias=eps[:, 0:1])
+
+        def normalise(k):
+            lo, hi = chunks[k]
+            ys[k] = work.tile([P, CB, hi - lo], F32, name="y")
+            for cb in range(CB):
+                normed = work.tile([P, hi - lo], F32, name="normed")
                 nc.vector.scalar_tensor_tensor(
-                    normed[:], zc[cb][:], bias_c[:, cb : cb + 1], rstd[:], op0=ALU.add, op1=ALU.mult
+                    normed[:], banks[k, cb][:], bias_c[cb], rstds[k][:], op0=ALU.add, op1=ALU.mult
                 )
-                y = work.tile([P, width], F32, name="y")
-                nc.scalar.activation(
-                    y[:], normed[:], ACT.Identity, bias=beta_col[:, cb : cb + 1], scale=gamma_col[:, cb : cb + 1]
-                )
-                leaky = work.tile([P, width], F32, name="leaky")
-                nc.vector.scalar_tensor_tensor(leaky[:], y[:], LEAKY_SLOPE, y[:], op0=ALU.mult, op1=ALU.max)
-                result = work.tile([P, width], F32, name="result")
-                nc.vector.tensor_add(result[:], leaky[:], h[cb][:, cols])
-                nc.sync.dma_start(out[cb * P : (cb + 1) * P, cols], result[:])
+                nc.scalar.activation(ys[k][:, cb, :], normed[:], ACT.Identity, bias=beta_col[cb], scale=gamma_col[cb])
+
+        def activate_and_store(k):
+            lo, hi = chunks[k]
+            leaky = work.tile([P, CB, hi - lo], F32, name="leaky")
+            nc.vector.scalar_tensor_tensor(leaky[:], ys[k][:], LEAKY_SLOPE, ys[k][:], op0=ALU.mult, op1=ALU.max)
+            result = work.tile([P, CB, hi - lo], F32, name="result")
+            nc.vector.tensor_add(result[:], leaky[:], h[:, :, lo:hi])
+            nc.sync.dma_start(out.rearrange("(cb p) j -> p cb j", p=P)[:, :, lo:hi], result[:])
+
+        for i in range(n_pieces):
+            look_up(0, i)
+        for k in range(CHUNKS_AHEAD):
+            project(k, wr_c, h_bf, 0)
+        sum_of_others(0, 0)
+        for i in range(n_pieces):
+            sum_of_others(0, i + 1)
+            look_up(1, i)
+        for k in range(CHUNKS_AHEAD):
+            project(k, wl_c, m_bf, 0)
+        for k in range(CHUNKS_AHEAD):
+            project(k, wr_c, h_bf, 1)
+        for k in range(n_chunks):
+            sum_of_others(1, k)
+        for k in range(CHUNKS_AHEAD):
+            project(k, wl_c, m_bf, 1)
+        reciprocal_std(0, variance(0))
+        for k in range(n_chunks):
+            if k + 1 < n_chunks:
+                next_var = variance(k + 1)
+            normalise(k)
+            if k + 1 < n_chunks:
+                reciprocal_std(k + 1, next_var)
+            activate_and_store(k)
+            if k + CHUNKS_AHEAD < n_chunks:
+                for weights, operand in ((wr_c, h_bf), (wl_c, m_bf)):
+                    for kb in range(CB):
+                        project(k + CHUNKS_AHEAD, weights, operand, kb)

@@ -21,6 +21,7 @@ LEAKY_SLOPE = 0.01
 FLOPS = 2 * 2 * C * C * N
 
 PIECE_NODES = (5, 4, 4, 4)
+GROUP = 4 * NICHES
 CHUNK_NODES = (2, 4, 4, 4, 3)
 CHUNKS_AHEAD = 3
 
@@ -56,7 +57,8 @@ def tile_gnnnicheencoder_kernel(tc, x, w_l, w_r, b_l, gamma, beta, offs, out):
         rows = held.tile([P, C], F32, name="rows")
         nc.vector.memset(rows[:], 0.0)
         for r, vec in enumerate(vectors):
-            nc.sync.dma_start(rows[r : r + 1, :], vec.rearrange("c o -> o c"))
+            queue = nc.sync if r == 0 else nc.scalar
+            queue.dma_start(rows[r : r + 1, :], vec.rearrange("c o -> o c"))
         wl_raw = held.tile([P, CB, C], BF16, name="wl_raw")
         wr_raw = held.tile([P, CB, C], BF16, name="wr_raw")
         nc.sync.dma_start(wl_raw[:], w_l.rearrange("(kb p) c -> p kb c", p=P))
@@ -102,19 +104,23 @@ def tile_gnnnicheencoder_kernel(tc, x, w_l, w_r, b_l, gamma, beta, offs, out):
         h = held.tile([P, CB, N], F32, name="h")
         h_bf = held.tile([P, CB, N], BF16, name="h_bf")
         m_bf = held.tile([P, CB, N], BF16, name="m_bf")
+        group_sum = held.tile([P, CB, GROUP], F32, name="group_sum")
+        pair_sum = held.tile([P, CB, GROUP // 2], F32, name="pair_sum")
         node_sum = held.tile([P, CB, NICHES], F32, name="node_sum")
 
         def look_up(cb, i):
             lo, hi = pieces[i]
             nc.scalar.activation(h[:, cb, lo:hi], store[cb][:].indirect(offsets[:, lo // 16 : hi // 16]), ACT.Copy)
             nc.gpsimd.tensor_copy(h_bf[:, cb, lo:hi], h[:, cb, lo:hi])
-            in_piece = h[:, cb, lo:hi].rearrange("p (n q) -> p q n", q=NICHES)
-            if i == 0:
-                nc.vector.tensor_reduce(node_sum[:, cb, :], in_piece, axis=AXIS_X, op=ALU.add)
-            else:
-                part = work.tile([P, NICHES], F32, name="part")
-                nc.vector.tensor_reduce(part[:], in_piece, axis=AXIS_X, op=ALU.add)
-                nc.vector.tensor_add(node_sum[:, cb, :], node_sum[:, cb, :], part[:])
+            total = group_sum[:, cb, :]
+            if i == 1:
+                nc.vector.tensor_add(total, h[:, cb, lo - GROUP : lo], h[:, cb, lo:hi])
+                nc.vector.tensor_add(total[:, 0:NICHES], total[:, 0:NICHES], h[:, cb, 0:NICHES])
+            if i > 1:
+                nc.vector.tensor_add(total, total, h[:, cb, lo:hi])
+            if i == n_pieces - 1:
+                nc.vector.tensor_add(pair_sum[:, cb, :], total[:, : GROUP // 2], total[:, GROUP // 2 :])
+                nc.vector.tensor_add(node_sum[:, cb, :], pair_sum[:, cb, :NICHES], pair_sum[:, cb, NICHES:])
 
         def sum_of_others(cb, k):
             lo, hi = chunks[k]

@@ -21,7 +21,6 @@ LEAKY_SLOPE = 0.01
 FLOPS = 2 * 2 * C * C * N
 
 PIECE_NODES = (5, 4, 4, 4)
-GROUP = 4 * NICHES
 CHUNK_NODES = (2, 4, 4, 4, 3)
 CHUNKS_AHEAD = 3
 
@@ -57,8 +56,7 @@ def tile_gnnnicheencoder_kernel(tc, x, w_l, w_r, b_l, gamma, beta, offs, out):
         rows = held.tile([P, C], F32, name="rows")
         nc.vector.memset(rows[:], 0.0)
         for r, vec in enumerate(vectors):
-            queue = nc.sync if r == 0 else nc.scalar
-            queue.dma_start(rows[r : r + 1, :], vec.rearrange("c o -> o c"))
+            nc.sync.dma_start(rows[r : r + 1, :], vec.rearrange("c o -> o c"))
         wl_raw = held.tile([P, CB, C], BF16, name="wl_raw")
         wr_raw = held.tile([P, CB, C], BF16, name="wr_raw")
         nc.sync.dma_start(wl_raw[:], w_l.rearrange("(kb p) c -> p kb c", p=P))
@@ -104,27 +102,25 @@ def tile_gnnnicheencoder_kernel(tc, x, w_l, w_r, b_l, gamma, beta, offs, out):
         h = held.tile([P, CB, N], F32, name="h")
         h_bf = held.tile([P, CB, N], BF16, name="h_bf")
         m_bf = held.tile([P, CB, N], BF16, name="m_bf")
-        group_sum = held.tile([P, CB, GROUP], F32, name="group_sum")
-        pair_sum = held.tile([P, CB, GROUP // 2], F32, name="pair_sum")
         node_sum = held.tile([P, CB, NICHES], F32, name="node_sum")
 
         def look_up(cb, i):
             lo, hi = pieces[i]
             nc.scalar.activation(h[:, cb, lo:hi], store[cb][:].indirect(offsets[:, lo // 16 : hi // 16]), ACT.Copy)
-            nc.gpsimd.tensor_copy(h_bf[:, cb, lo:hi], h[:, cb, lo:hi])
-            total = group_sum[:, cb, :]
-            if i == 1:
-                nc.vector.tensor_add(total, h[:, cb, lo - GROUP : lo], h[:, cb, lo:hi])
-                nc.vector.tensor_add(total[:, 0:NICHES], total[:, 0:NICHES], h[:, cb, 0:NICHES])
-            if i > 1:
-                nc.vector.tensor_add(total, total, h[:, cb, lo:hi])
-            if i == n_pieces - 1:
-                nc.vector.tensor_add(pair_sum[:, cb, :], total[:, : GROUP // 2], total[:, GROUP // 2 :])
-                nc.vector.tensor_add(node_sum[:, cb, :], pair_sum[:, cb, :NICHES], pair_sum[:, cb, NICHES:])
+            caster = nc.gpsimd if cb == 0 else nc.vector
+            caster.tensor_copy(h_bf[:, cb, lo:hi], h[:, cb, lo:hi])
+            in_piece = h[:, cb, lo:hi].rearrange("p (n q) -> p q n", q=NICHES)
+            if i == 0:
+                nc.vector.tensor_reduce(node_sum[:, cb, :], in_piece, axis=AXIS_X, op=ALU.add)
+            else:
+                part = work.tile([P, NICHES], F32, name="part")
+                nc.vector.tensor_reduce(part[:], in_piece, axis=AXIS_X, op=ALU.add)
+                nc.vector.tensor_add(node_sum[:, cb, :], node_sum[:, cb, :], part[:])
 
         def sum_of_others(cb, k):
             lo, hi = chunks[k]
-            nc.vector.tensor_sub(
+            engine = nc.vector if cb == CB - 1 and k < CHUNKS_AHEAD else nc.gpsimd
+            engine.tensor_sub(
                 by_node(m_bf[:, cb, lo:hi]),
                 node_sum[:, cb, :].unsqueeze(1).to_broadcast([P, CHUNK_NODES[k], NICHES]),
                 by_node(h[:, cb, lo:hi]),
@@ -178,7 +174,8 @@ def tile_gnnnicheencoder_kernel(tc, x, w_l, w_r, b_l, gamma, beta, offs, out):
             leaky = work.tile([P, CB, hi - lo], F32, name="leaky")
             nc.vector.scalar_tensor_tensor(leaky[:], ys[k][:], LEAKY_SLOPE, ys[k][:], op0=ALU.mult, op1=ALU.max)
             result = work.tile([P, CB, hi - lo], F32, name="result")
-            nc.vector.tensor_add(result[:], leaky[:], h[:, :, lo:hi])
+            adder = nc.gpsimd if k % 2 == 1 else nc.vector
+            adder.tensor_add(result[:], leaky[:], h[:, :, lo:hi])
             nc.sync.dma_start(out.rearrange("(cb p) j -> p cb j", p=P)[:, :, lo:hi], result[:])
 
         for i in range(n_pieces):

@@ -107,42 +107,40 @@ def tile_gnnnicheencoder_kernel(tc, x, w_l, w_r, b_l, gamma, beta, offs, out):
         def look_up(cb, i):
             lo, hi = pieces[i]
             nc.scalar.activation(h[:, cb, lo:hi], store[cb][:].indirect(offsets[:, lo // 16 : hi // 16]), ACT.Copy)
-            caster = nc.gpsimd if cb == 0 else nc.vector
-            caster.tensor_copy(h_bf[:, cb, lo:hi], h[:, cb, lo:hi])
-            in_piece = h[:, cb, lo:hi].rearrange("p (n q) -> p q n", q=NICHES)
+            nc.gpsimd.tensor_copy(h_bf[:, cb, lo:hi], h[:, cb, lo:hi])
+            nodes_last = h[:, cb, lo:hi].rearrange("p (n q) -> p q n", q=NICHES)
             if i == 0:
-                nc.vector.tensor_reduce(node_sum[:, cb, :], in_piece, axis=AXIS_X, op=ALU.add)
+                nc.vector.tensor_reduce(node_sum[:, cb, :], nodes_last, axis=AXIS_X, op=ALU.add)
             else:
                 part = work.tile([P, NICHES], F32, name="part")
-                nc.vector.tensor_reduce(part[:], in_piece, axis=AXIS_X, op=ALU.add)
+                nc.vector.tensor_reduce(part[:], nodes_last, axis=AXIS_X, op=ALU.add)
                 nc.vector.tensor_add(node_sum[:, cb, :], node_sum[:, cb, :], part[:])
 
         def sum_of_others(cb, k):
             lo, hi = chunks[k]
-            engine = nc.vector if cb == CB - 1 and k < CHUNKS_AHEAD else nc.gpsimd
-            engine.tensor_sub(
+            nc.vector.tensor_sub(
                 by_node(m_bf[:, cb, lo:hi]),
                 node_sum[:, cb, :].unsqueeze(1).to_broadcast([P, CHUNK_NODES[k], NICHES]),
                 by_node(h[:, cb, lo:hi]),
             )
 
+        products = ((wr_c, h_bf, 0), (wl_c, m_bf, 0), (wr_c, h_bf, 1), (wl_c, m_bf, 1))
         banks = {}
         rstds = {}
         ys = {}
 
-        def project(k, weights, operand, kb):
+        def project(k, step):
             lo, hi = chunks[k]
-            opens = weights is wr_c and kb == 0
-            closes = weights is wl_c and kb == CB - 1
+            weights, operand, kb = products[step]
             for cb in range(CB):
-                if opens:
+                if step == 0:
                     banks[k, cb] = psum.tile([P, hi - lo], F32, name=f"zc{cb}", bufs=CHUNKS_AHEAD)
                 nc.tensor.matmul(
                     banks[k, cb][:],
                     weights[:, kb, cb * P : (cb + 1) * P],
                     operand[:, kb, lo:hi],
-                    start=opens,
-                    stop=closes,
+                    start=(step == 0),
+                    stop=(step == len(products) - 1),
                 )
 
         def variance(k):
@@ -174,26 +172,17 @@ def tile_gnnnicheencoder_kernel(tc, x, w_l, w_r, b_l, gamma, beta, offs, out):
             leaky = work.tile([P, CB, hi - lo], F32, name="leaky")
             nc.vector.scalar_tensor_tensor(leaky[:], ys[k][:], LEAKY_SLOPE, ys[k][:], op0=ALU.mult, op1=ALU.max)
             result = work.tile([P, CB, hi - lo], F32, name="result")
-            adder = nc.gpsimd if k % 2 == 1 else nc.vector
-            adder.tensor_add(result[:], leaky[:], h[:, :, lo:hi])
+            nc.vector.tensor_add(result[:], leaky[:], h[:, :, lo:hi])
             nc.sync.dma_start(out.rearrange("(cb p) j -> p cb j", p=P)[:, :, lo:hi], result[:])
 
-        for i in range(n_pieces):
-            look_up(0, i)
-        for k in range(CHUNKS_AHEAD):
-            project(k, wr_c, h_bf, 0)
-        sum_of_others(0, 0)
-        for i in range(n_pieces):
-            sum_of_others(0, i + 1)
-            look_up(1, i)
-        for k in range(CHUNKS_AHEAD):
-            project(k, wl_c, m_bf, 0)
-        for k in range(CHUNKS_AHEAD):
-            project(k, wr_c, h_bf, 1)
-        for k in range(n_chunks):
-            sum_of_others(1, k)
-        for k in range(CHUNKS_AHEAD):
-            project(k, wl_c, m_bf, 1)
+        for cb in range(CB):
+            for i in range(n_pieces):
+                look_up(cb, i)
+            for k in range(n_chunks):
+                sum_of_others(cb, k)
+        for step in range(len(products)):
+            for k in range(CHUNKS_AHEAD):
+                project(k, step)
         reciprocal_std(0, variance(0))
         for k in range(n_chunks):
             if k + 1 < n_chunks:
@@ -203,6 +192,5 @@ def tile_gnnnicheencoder_kernel(tc, x, w_l, w_r, b_l, gamma, beta, offs, out):
                 reciprocal_std(k + 1, next_var)
             activate_and_store(k)
             if k + CHUNKS_AHEAD < n_chunks:
-                for weights, operand in ((wr_c, h_bf), (wl_c, m_bf)):
-                    for kb in range(CB):
-                        project(k + CHUNKS_AHEAD, weights, operand, kb)
+                for step in range(len(products)):
+                    project(k + CHUNKS_AHEAD, step)

@@ -107,7 +107,7 @@ def tile_gnnnicheencoder_kernel(tc, x, w_l, w_r, b_l, gamma, beta, offs, out):
         def look_up(cb, i):
             lo, hi = pieces[i]
             nc.scalar.activation(h[:, cb, lo:hi], store[cb][:].indirect(offsets[:, lo // 16 : hi // 16]), ACT.Copy)
-            nc.gpsimd.tensor_copy(h_bf[:, cb, lo:hi], h[:, cb, lo:hi])
+            nc.vector.tensor_copy(h_bf[:, cb, lo:hi], h[:, cb, lo:hi])
             nodes_last = h[:, cb, lo:hi].rearrange("p (n q) -> p q n", q=NICHES)
             if i == 0:
                 nc.vector.tensor_reduce(node_sum[:, cb, :], nodes_last, axis=AXIS_X, op=ALU.add)

@@ -20,7 +20,7 @@ LEAKY_SLOPE = 0.01
 
 FLOPS = 2 * 2 * C * C * N
 
-PIECE_NODES = (5, 4, 4, 4)
+PIECE_NODES = (4, 4, 4, 4, 1)
 CHUNK_NODES = (2, 4, 4, 4, 3)
 CHUNKS_AHEAD = 3
 
@@ -51,20 +51,23 @@ def tile_gnnnicheencoder_kernel(tc, x, w_l, w_r, b_l, gamma, beta, offs, out):
     ):
         offsets = held.tile([P, N // 16], U16, name="offsets")
         nc.sync.dma_start(offsets[:], offs)
+        store = [held.tile([P, S], F32, name=f"store{cb}") for cb in range(CB)]
 
+        def load_window(cb):
+            nc.sync.dma_start(store[cb][:, : S // 2], x[cb * P : (cb + 1) * P, : S // 2])
+            nc.scalar.dma_start(store[cb][:, S // 2 :], x[cb * P : (cb + 1) * P, S // 2 :])
+
+        load_window(0)
+        wl_raw = held.tile([P, CB, C], BF16, name="wl_raw")
+        wr_raw = held.tile([P, CB, C], BF16, name="wr_raw")
+        nc.sync.dma_start(wl_raw[:], w_l.rearrange("(kb p) c -> p kb c", p=P))
+        nc.scalar.dma_start(wr_raw[:], w_r.rearrange("(kb p) c -> p kb c", p=P))
         vectors = (b_l, gamma, beta)
         rows = held.tile([P, C], F32, name="rows")
         nc.vector.memset(rows[:], 0.0)
         for r, vec in enumerate(vectors):
             nc.sync.dma_start(rows[r : r + 1, :], vec.rearrange("c o -> o c"))
-        wl_raw = held.tile([P, CB, C], BF16, name="wl_raw")
-        wr_raw = held.tile([P, CB, C], BF16, name="wr_raw")
-        nc.sync.dma_start(wl_raw[:], w_l.rearrange("(kb p) c -> p kb c", p=P))
-        nc.scalar.dma_start(wr_raw[:], w_r.rearrange("(kb p) c -> p kb c", p=P))
-        store = [held.tile([P, S], F32, name=f"store{cb}") for cb in range(CB)]
-        for cb in range(CB):
-            nc.sync.dma_start(store[cb][:, : S // 2], x[cb * P : (cb + 1) * P, : S // 2])
-            nc.scalar.dma_start(store[cb][:, S // 2 :], x[cb * P : (cb + 1) * P, S // 2 :])
+        load_window(1)
 
         mean_mat = held.tile([P, P], BF16, name="mean_mat")
         nc.vector.memset(mean_mat[:], 1.0 / C)
@@ -72,6 +75,8 @@ def tile_gnnnicheencoder_kernel(tc, x, w_l, w_r, b_l, gamma, beta, offs, out):
         nc.vector.memset(eps[:], LN_EPS)
         identity = held.tile([P, P], F32, name="identity")
         make_identity(nc, identity[:])
+        identity_bf = held.tile([P, P], BF16, name="identity_bf")
+        nc.vector.tensor_copy(identity_bf[:], identity[:])
         warm = held.tile([P, 1], F32, name="warm")
         nc.scalar.activation(warm[:], eps[:], ACT.Abs_reciprocal_sqrt)
 
@@ -85,112 +90,144 @@ def tile_gnnnicheencoder_kernel(tc, x, w_l, w_r, b_l, gamma, beta, offs, out):
         columns = held.tile([P, CB, len(vectors)], F32, name="columns")
         nc.vector.tensor_copy(columns[:], turned[:, :, 0 : len(vectors)])
         bias_c = [columns[:, cb, 0:1] for cb in range(CB)]
-        gamma_col = [columns[:, cb, 1:2] for cb in range(CB)]
-        beta_col = [columns[:, cb, 2:3] for cb in range(CB)]
+        relu_scaled = held.tile([P, CB, 2], F32, name="relu_scaled")
+        nc.vector.tensor_scalar_mul(relu_scaled[:], columns[:, :, 1:3], 1.0 - LEAKY_SLOPE)
+        line_scaled = held.tile([P, CB, 2], F32, name="line_scaled")
+        nc.vector.tensor_scalar_mul(line_scaled[:], columns[:, :, 1:3], LEAKY_SLOPE)
 
-        wl_c = held.tile([P, CB, C], BF16, name="wl_c")
-        wr_c = held.tile([P, CB, C], BF16, name="wr_c")
-        for raw, centred, factor, side in ((wl_raw, wl_c, 1.0 / (NODES - 1), "l"), (wr_raw, wr_c, 1.0, "r")):
-            neg_mean = held.tile([P, CB], F32, name=f"neg_mean_{side}")
-            nc.vector.tensor_reduce(neg_mean[:], raw[:], axis=AXIS_X, op=ALU.add)
-            nc.vector.tensor_scalar_mul(neg_mean[:], neg_mean[:], -1.0 / C)
-            for kb in range(CB):
-                nc.vector.tensor_scalar(
-                    centred[:, kb, :], raw[:, kb, :], neg_mean[:, kb : kb + 1], factor, op0=ALU.add, op1=ALU.mult
-                )
+        neg_mean = {}
+        for raw, side in ((wl_raw, "l"), (wr_raw, "r")):
+            neg_mean[side] = held.tile([P, CB], F32, name=f"neg_mean_{side}")
+            nc.vector.tensor_reduce(neg_mean[side][:], raw[:], axis=AXIS_X, op=ALU.add)
+            nc.vector.tensor_scalar_mul(neg_mean[side][:], neg_mean[side][:], -1.0 / C)
+        wl_16 = held.tile([P, CB, C], F32, name="wl_16")
+        w_sum = held.tile([P, CB, C], BF16, name="w_sum")
+        w_own = held.tile([P, CB, C], BF16, name="w_own")
+        for kb in range(CB):
+            nc.vector.tensor_scalar(
+                wl_16[:, kb, :], wl_raw[:, kb, :], neg_mean["l"][:, kb : kb + 1], 1.0 / (NODES - 1),
+                op0=ALU.add, op1=ALU.mult,
+            )
+            nc.vector.tensor_copy(w_sum[:, kb, :], wl_16[:, kb, :])
+            nc.vector.scalar_tensor_tensor(
+                w_own[:, kb, :], wr_raw[:, kb, :], neg_mean["r"][:, kb : kb + 1], wl_16[:, kb, :],
+                op0=ALU.add, op1=ALU.subtract,
+            )
 
         h = held.tile([P, CB, N], F32, name="h")
         h_bf = held.tile([P, CB, N], BF16, name="h_bf")
-        m_bf = held.tile([P, CB, N], BF16, name="m_bf")
-        node_sum = held.tile([P, CB, NICHES], F32, name="node_sum")
+        h_beta = held.tile([P, CB, N], F32, name="h_beta")
+        sum_term = psum.tile([P, CB, NICHES], F32, name="sum_term", tag="var", bufs=2)
+        sum_bf = held.tile([P, CB, NICHES], BF16, name="sum_bf")
 
-        def look_up(cb, i):
+        def look_up(kb, i):
             lo, hi = pieces[i]
-            nc.scalar.activation(h[:, cb, lo:hi], store[cb][:].indirect(offsets[:, lo // 16 : hi // 16]), ACT.Copy)
-            nc.vector.tensor_copy(h_bf[:, cb, lo:hi], h[:, cb, lo:hi])
-            nodes_last = h[:, cb, lo:hi].rearrange("p (n q) -> p q n", q=NICHES)
-            if i == 0:
-                nc.vector.tensor_reduce(node_sum[:, cb, :], nodes_last, axis=AXIS_X, op=ALU.add)
-            else:
-                part = work.tile([P, NICHES], F32, name="part")
-                nc.vector.tensor_reduce(part[:], nodes_last, axis=AXIS_X, op=ALU.add)
-                nc.vector.tensor_add(node_sum[:, cb, :], node_sum[:, cb, :], part[:])
-
-        def sum_of_others(cb, k):
-            lo, hi = chunks[k]
-            nc.vector.tensor_sub(
-                by_node(m_bf[:, cb, lo:hi]),
-                node_sum[:, cb, :].unsqueeze(1).to_broadcast([P, CHUNK_NODES[k], NICHES]),
-                by_node(h[:, cb, lo:hi]),
-            )
-
-        products = ((wr_c, h_bf, 0), (wl_c, m_bf, 0), (wr_c, h_bf, 1), (wl_c, m_bf, 1))
-        banks = {}
-        rstds = {}
-        ys = {}
-
-        def project(k, step):
-            lo, hi = chunks[k]
-            weights, operand, kb = products[step]
+            nc.scalar.activation(h[:, kb, lo:hi], store[kb][:].indirect(offsets[:, lo // 16 : hi // 16]), ACT.Copy)
+            nc.vector.tensor_copy(h_bf[:, kb, lo:hi], h[:, kb, lo:hi])
             for cb in range(CB):
-                if step == 0:
+                for node_lo in range(lo, hi, NICHES):
+                    nc.tensor.matmul(
+                        sum_term[:, cb, :],
+                        w_sum[:, kb, cb * P : (cb + 1) * P],
+                        h_bf[:, kb, node_lo : node_lo + NICHES],
+                        start=(kb == 0 and cb == 0 and node_lo == 0),
+                        stop=(kb == CB - 1 and cb == CB - 1 and node_lo == N - NICHES),
+                    )
+            nc.vector.tensor_scalar_add(h_beta[:, kb, lo:hi], h[:, kb, lo:hi], line_scaled[:, kb, 1:2])
+
+        banks = {}
+        variances = {}
+        rstds = {}
+        normed = {}
+        relu_parts = {}
+        line_parts = {}
+
+        def project(k, kb):
+            lo, hi = chunks[k]
+            for cb in range(CB):
+                if kb == 0:
                     banks[k, cb] = psum.tile([P, hi - lo], F32, name=f"zc{cb}", bufs=CHUNKS_AHEAD)
                 nc.tensor.matmul(
-                    banks[k, cb][:],
-                    weights[:, kb, cb * P : (cb + 1) * P],
-                    operand[:, kb, lo:hi],
-                    start=(step == 0),
-                    stop=(step == len(products) - 1),
+                    banks[k, cb][:], w_own[:, kb, cb * P : (cb + 1) * P], h_bf[:, kb, lo:hi], start=(kb == 0), stop=False
+                )
+
+        def add_sum_term(k):
+            for cb in range(CB):
+                nc.tensor.matmul(
+                    by_node(banks[k, cb][:]),
+                    identity_bf[:],
+                    sum_bf[:, cb, :].unsqueeze(1).to_broadcast([P, CHUNK_NODES[k], NICHES]),
+                    start=False,
+                    stop=True,
                 )
 
         def variance(k):
             lo, hi = chunks[k]
-            var = psum.tile([P, hi - lo], F32, name="var", bufs=2)
+            variances[k] = psum.tile([P, hi - lo], F32, name="var", bufs=2)
             for cb in range(CB):
                 sq = work.tile([P, hi - lo], BF16, name="sq")
                 nc.scalar.activation(sq[:], banks[k, cb][:], ACT.Square, bias=bias_c[cb])
-                nc.tensor.matmul(var[:], mean_mat[:], sq[:], start=(cb == 0), stop=(cb == CB - 1))
-            return var
+                nc.tensor.matmul(variances[k][:], mean_mat[:], sq[:], start=(cb == 0), stop=(cb == CB - 1))
 
-        def reciprocal_std(k, var):
+        def reciprocal_std(k):
             lo, hi = chunks[k]
             rstds[k] = work.tile([P, hi - lo], F32, name="rstd")
-            nc.scalar.activation(rstds[k][:], var[:], ACT.Abs_reciprocal_sqrt, bias=eps[:, 0:1])
+            nc.scalar.activation(rstds[k][:], variances[k][:], ACT.Abs_reciprocal_sqrt, bias=eps[:, 0:1])
 
         def normalise(k):
             lo, hi = chunks[k]
-            ys[k] = work.tile([P, CB, hi - lo], F32, name="y")
+            normed[k] = work.tile([P, CB, hi - lo], F32, name="normed")
             for cb in range(CB):
-                normed = work.tile([P, hi - lo], F32, name="normed")
                 nc.vector.scalar_tensor_tensor(
-                    normed[:], banks[k, cb][:], bias_c[cb], rstds[k][:], op0=ALU.add, op1=ALU.mult
+                    normed[k][:, cb, :], banks[k, cb][:], bias_c[cb], rstds[k][:], op0=ALU.add, op1=ALU.mult
                 )
-                nc.scalar.activation(ys[k][:, cb, :], normed[:], ACT.Identity, bias=beta_col[cb], scale=gamma_col[cb])
 
-        def activate_and_store(k):
+        def relu_part(k):
             lo, hi = chunks[k]
-            leaky = work.tile([P, CB, hi - lo], F32, name="leaky")
-            nc.vector.scalar_tensor_tensor(leaky[:], ys[k][:], LEAKY_SLOPE, ys[k][:], op0=ALU.mult, op1=ALU.max)
+            relu_parts[k] = work.tile([P, CB, hi - lo], F32, name="relu_part")
+            for cb in range(CB):
+                nc.scalar.activation(
+                    relu_parts[k][:, cb, :], normed[k][:, cb, :], ACT.Relu,
+                    bias=relu_scaled[:, cb, 1:2], scale=relu_scaled[:, cb, 0:1],
+                )
+
+        def line_part(k):
+            lo, hi = chunks[k]
+            line_parts[k] = work.tile([P, CB, hi - lo], F32, name="line_part")
+            for cb in range(CB):
+                nc.vector.scalar_tensor_tensor(
+                    line_parts[k][:, cb, :], normed[k][:, cb, :], line_scaled[:, cb, 0:1], h_beta[:, cb, lo:hi],
+                    op0=ALU.mult, op1=ALU.add,
+                )
+
+        def add_and_store(k):
+            lo, hi = chunks[k]
             result = work.tile([P, CB, hi - lo], F32, name="result")
-            nc.vector.tensor_add(result[:], leaky[:], h[:, :, lo:hi])
+            nc.vector.tensor_add(result[:], line_parts[k][:], relu_parts[k][:])
             nc.sync.dma_start(out.rearrange("(cb p) j -> p cb j", p=P)[:, :, lo:hi], result[:])
 
-        for cb in range(CB):
+        for kb in range(CB):
             for i in range(n_pieces):
-                look_up(cb, i)
-            for k in range(n_chunks):
-                sum_of_others(cb, k)
-        for step in range(len(products)):
+                look_up(kb, i)
+        for kb in range(CB):
             for k in range(CHUNKS_AHEAD):
-                project(k, step)
-        reciprocal_std(0, variance(0))
+                project(k, kb)
+        nc.vector.tensor_copy(sum_bf[:], sum_term[:])
+        for k in range(CHUNKS_AHEAD):
+            add_sum_term(k)
+        variance(0)
+        variance(1)
+        reciprocal_std(0)
         for k in range(n_chunks):
-            if k + 1 < n_chunks:
-                next_var = variance(k + 1)
             normalise(k)
-            if k + 1 < n_chunks:
-                reciprocal_std(k + 1, next_var)
-            activate_and_store(k)
             if k + CHUNKS_AHEAD < n_chunks:
-                for step in range(len(products)):
-                    project(k + CHUNKS_AHEAD, step)
+                for kb in range(CB):
+                    project(k + CHUNKS_AHEAD, kb)
+                add_sum_term(k + CHUNKS_AHEAD)
+            if k + 1 < n_chunks:
+                reciprocal_std(k + 1)
+            relu_part(k)
+            line_part(k)
+            if k + 2 < n_chunks:
+                variance(k + 2)
+            add_and_store(k)

@@ -21,7 +21,7 @@ LEAKY_SLOPE = 0.01
 FLOPS = 2 * 2 * C * C * N
 
 PIECE_NODES = (4, 4, 4, 4, 1)
-CHUNK_NODES = (2, 4, 4, 4, 3)
+CHUNK_NODES = (1, 2, 3, 4, 4, 3)
 CHUNKS_AHEAD = 3
 
 

@@ -21,7 +21,7 @@ LEAKY_SLOPE = 0.01
 FLOPS = 2 * 2 * C * C * N
 
 PIECE_NODES = (4, 4, 4, 4, 1)
-CHUNK_NODES = (1, 2, 3, 4, 4, 3)
+CHUNK_NODES = (1, 2, 3, 4, 4, 2, 1)
 CHUNKS_AHEAD = 3
 
 
@@ -52,22 +52,19 @@ def tile_gnnnicheencoder_kernel(tc, x, w_l, w_r, b_l, gamma, beta, offs, out):
         offsets = held.tile([P, N // 16], U16, name="offsets")
         nc.sync.dma_start(offsets[:], offs)
         store = [held.tile([P, S], F32, name=f"store{cb}") for cb in range(CB)]
-
-        def load_window(cb):
-            nc.sync.dma_start(store[cb][:, : S // 2], x[cb * P : (cb + 1) * P, : S // 2])
-            nc.scalar.dma_start(store[cb][:, S // 2 :], x[cb * P : (cb + 1) * P, S // 2 :])
-
-        load_window(0)
+        for cb in range(CB):
+            for half in range(2):
+                cells = slice(half * S // 2, (half + 1) * S // 2)
+                nc.sync.dma_start(store[cb][:, cells], x[cb * P : (cb + 1) * P, cells])
         wl_raw = held.tile([P, CB, C], BF16, name="wl_raw")
         wr_raw = held.tile([P, CB, C], BF16, name="wr_raw")
-        nc.sync.dma_start(wl_raw[:], w_l.rearrange("(kb p) c -> p kb c", p=P))
+        nc.scalar.dma_start(wl_raw[:], w_l.rearrange("(kb p) c -> p kb c", p=P))
         nc.scalar.dma_start(wr_raw[:], w_r.rearrange("(kb p) c -> p kb c", p=P))
         vectors = (b_l, gamma, beta)
         rows = held.tile([P, C], F32, name="rows")
         nc.vector.memset(rows[:], 0.0)
         for r, vec in enumerate(vectors):
-            nc.sync.dma_start(rows[r : r + 1, :], vec.rearrange("c o -> o c"))
-        load_window(1)
+            nc.scalar.dma_start(rows[r : r + 1, :], vec.rearrange("c o -> o c"))
 
         mean_mat = held.tile([P, P], BF16, name="mean_mat")
         nc.vector.memset(mean_mat[:], 1.0 / C)

@@ -21,28 +21,24 @@ LEAKY_SLOPE = 0.01
 FLOPS = 2 * 2 * C * C * N
 
 PIECE_NODES = (4, 4, 4, 4, 1)
-CHUNK_NODES = (1, 2, 3, 4, 4, 2, 1)
-CHUNKS_AHEAD = 3
+CHUNK_NODES = (1, 2, 2, 2, 2, 2, 2, 2, 2)
+Z_BANKS = 4
+T_BANKS = 3
 
 
-def spans(node_counts):
-    ranges = []
+def node_spans(node_counts):
+    spans = []
     first = 0
     for nodes in node_counts:
-        ranges.append((first * NICHES, (first + nodes) * NICHES))
+        spans.append((first, first + nodes))
         first += nodes
-    return ranges
-
-
-def by_node(ap):
-    return ap.rearrange("p (n q) -> p n q", q=NICHES)
+    return spans
 
 
 def tile_gnnnicheencoder_kernel(tc, x, w_l, w_r, b_l, gamma, beta, offs, out):
     nc = tc.nc
-    pieces = spans(PIECE_NODES)
-    chunks = spans(CHUNK_NODES)
-    n_pieces = len(pieces)
+    pieces = node_spans(PIECE_NODES)
+    chunks = node_spans(CHUNK_NODES)
     n_chunks = len(chunks)
     with (
         tc.tile_pool(name="held", bufs=1) as held,
@@ -66,14 +62,15 @@ def tile_gnnnicheencoder_kernel(tc, x, w_l, w_r, b_l, gamma, beta, offs, out):
         for r, vec in enumerate(vectors):
             nc.scalar.dma_start(rows[r : r + 1, :], vec.rearrange("c o -> o c"))
 
-        mean_mat = held.tile([P, P], BF16, name="mean_mat")
-        nc.vector.memset(mean_mat[:], 1.0 / C)
         eps = held.tile([P, 1], F32, name="eps")
         nc.vector.memset(eps[:], LN_EPS)
         identity = held.tile([P, P], F32, name="identity")
         make_identity(nc, identity[:])
         identity_bf = held.tile([P, P], BF16, name="identity_bf")
         nc.vector.tensor_copy(identity_bf[:], identity[:])
+        spread_row0 = held.tile([P, P], F32, name="spread_row0")
+        nc.vector.memset(spread_row0[:], 0.0)
+        nc.vector.memset(spread_row0[0:1, :], 1.0)
         warm = held.tile([P, 1], F32, name="warm")
         nc.scalar.activation(warm[:], eps[:], ACT.Abs_reciprocal_sqrt)
 
@@ -81,16 +78,17 @@ def tile_gnnnicheencoder_kernel(tc, x, w_l, w_r, b_l, gamma, beta, offs, out):
         nc.vector.tensor_reduce(neg_bias_mean[:], rows[0:1, :], axis=AXIS_X, op=ALU.add)
         nc.vector.tensor_scalar_mul(neg_bias_mean[:], neg_bias_mean[:], -1.0 / C)
         nc.vector.tensor_scalar_add(rows[0:1, :], rows[0:1, :], neg_bias_mean[:])
-        turned = psum.tile([P, CB, P], F32, name="turned", tag="var", bufs=2)
+        bias_spread = psum.tile([P, C], F32, name="bias_spread", tag="sum_term")
+        nc.tensor.matmul(bias_spread[:], spread_row0[:], rows[:], start=True, stop=True)
+        bias_rows = held.tile([P, C], F32, name="bias_rows")
+        nc.vector.tensor_copy(bias_rows[:], bias_spread[:])
+        turned = psum.tile([P, CB, P], F32, name="turned", tag="sum_term")
         for cb in range(CB):
             nc.tensor.transpose(turned[:, cb, :], rows[:, cb * P : (cb + 1) * P], identity[:])
-        columns = held.tile([P, CB, len(vectors)], F32, name="columns")
-        nc.vector.tensor_copy(columns[:], turned[:, :, 0 : len(vectors)])
-        bias_c = [columns[:, cb, 0:1] for cb in range(CB)]
         relu_scaled = held.tile([P, CB, 2], F32, name="relu_scaled")
-        nc.vector.tensor_scalar_mul(relu_scaled[:], columns[:, :, 1:3], 1.0 - LEAKY_SLOPE)
+        nc.vector.tensor_scalar_mul(relu_scaled[:], turned[:, :, 1:3], 1.0 - LEAKY_SLOPE)
         line_scaled = held.tile([P, CB, 2], F32, name="line_scaled")
-        nc.vector.tensor_scalar_mul(line_scaled[:], columns[:, :, 1:3], LEAKY_SLOPE)
+        nc.vector.tensor_scalar_mul(line_scaled[:], turned[:, :, 1:3], LEAKY_SLOPE)
 
         neg_mean = {}
         for raw, side in ((wl_raw, "l"), (wr_raw, "r")):
@@ -114,117 +112,131 @@ def tile_gnnnicheencoder_kernel(tc, x, w_l, w_r, b_l, gamma, beta, offs, out):
         h = held.tile([P, CB, N], F32, name="h")
         h_bf = held.tile([P, CB, N], BF16, name="h_bf")
         h_beta = held.tile([P, CB, N], F32, name="h_beta")
-        sum_term = psum.tile([P, CB, NICHES], F32, name="sum_term", tag="var", bufs=2)
-        sum_bf = held.tile([P, CB, NICHES], BF16, name="sum_bf")
+        sum_term = psum.tile([P, C], F32, name="sum_term")
+        sum_bf = held.tile([P, C], BF16, name="sum_bf")
+        square_sums = held.tile([P, NODES], F32, name="square_sums")
+        rstd = held.tile([P, NODES], F32, name="rstd")
+
+        def node_of(tile, kb, node):
+            return tile[:, kb, node * NICHES : (node + 1) * NICHES]
 
         def look_up(kb, i):
-            lo, hi = pieces[i]
+            first, end = pieces[i]
+            lo, hi = first * NICHES, end * NICHES
             nc.scalar.activation(h[:, kb, lo:hi], store[kb][:].indirect(offsets[:, lo // 16 : hi // 16]), ACT.Copy)
             nc.vector.tensor_copy(h_bf[:, kb, lo:hi], h[:, kb, lo:hi])
-            for cb in range(CB):
-                for node_lo in range(lo, hi, NICHES):
-                    nc.tensor.matmul(
-                        sum_term[:, cb, :],
-                        w_sum[:, kb, cb * P : (cb + 1) * P],
-                        h_bf[:, kb, node_lo : node_lo + NICHES],
-                        start=(kb == 0 and cb == 0 and node_lo == 0),
-                        stop=(kb == CB - 1 and cb == CB - 1 and node_lo == N - NICHES),
-                    )
+            for node in range(first, end):
+                nc.tensor.matmul(
+                    sum_term[:],
+                    node_of(h_bf, kb, node),
+                    w_sum[:, kb, :],
+                    start=(kb == 0 and node == 0),
+                    stop=(kb == CB - 1 and node == NODES - 1),
+                )
             nc.vector.tensor_scalar_add(h_beta[:, kb, lo:hi], h[:, kb, lo:hi], line_scaled[:, kb, 1:2])
 
-        banks = {}
-        variances = {}
-        rstds = {}
+        z_banks = {}
         normed = {}
+        t_banks = {}
         relu_parts = {}
         line_parts = {}
 
         def project(k, kb):
-            lo, hi = chunks[k]
-            for cb in range(CB):
-                if kb == 0:
-                    banks[k, cb] = psum.tile([P, hi - lo], F32, name=f"zc{cb}", bufs=CHUNKS_AHEAD)
+            first, end = chunks[k]
+            if kb == 0:
+                z_banks[k] = psum.tile([P, end - first, C], F32, name="z_bank", bufs=Z_BANKS)
+            for node in range(first, end):
                 nc.tensor.matmul(
-                    banks[k, cb][:], w_own[:, kb, cb * P : (cb + 1) * P], h_bf[:, kb, lo:hi], start=(kb == 0), stop=False
+                    z_banks[k][:, node - first, :],
+                    node_of(h_bf, kb, node),
+                    w_own[:, kb, :],
+                    start=(kb == 0 and node == first),
+                    stop=False,
                 )
 
         def add_sum_term(k):
-            for cb in range(CB):
-                nc.tensor.matmul(
-                    by_node(banks[k, cb][:]),
-                    identity_bf[:],
-                    sum_bf[:, cb, :].unsqueeze(1).to_broadcast([P, CHUNK_NODES[k], NICHES]),
-                    start=False,
-                    stop=True,
-                )
-
-        def variance(k):
-            lo, hi = chunks[k]
-            variances[k] = psum.tile([P, hi - lo], F32, name="var", bufs=2)
-            for cb in range(CB):
-                sq = work.tile([P, hi - lo], BF16, name="sq")
-                nc.scalar.activation(sq[:], banks[k, cb][:], ACT.Square, bias=bias_c[cb])
-                nc.tensor.matmul(variances[k][:], mean_mat[:], sq[:], start=(cb == 0), stop=(cb == CB - 1))
+            first, end = chunks[k]
+            nc.tensor.matmul(
+                z_banks[k][:],
+                identity_bf[:],
+                sum_bf[:].unsqueeze(1).to_broadcast([P, end - first, C]),
+                start=False,
+                stop=True,
+            )
 
         def reciprocal_std(k):
-            lo, hi = chunks[k]
-            rstds[k] = work.tile([P, hi - lo], F32, name="rstd")
-            nc.scalar.activation(rstds[k][:], variances[k][:], ACT.Abs_reciprocal_sqrt, bias=eps[:, 0:1])
+            first, end = chunks[k]
+            for node in range(first, end):
+                squares = work.tile([P, C], BF16, name="squares")
+                nc.scalar.activation(
+                    squares[:], z_banks[k][:, node - first, :], ACT.Square, accum_out=square_sums[:, node : node + 1]
+                )
+            nc.scalar.activation(
+                rstd[:, first:end], square_sums[:, first:end], ACT.Abs_reciprocal_sqrt, bias=eps[:, 0:1], scale=1.0 / C
+            )
 
         def normalise(k):
-            lo, hi = chunks[k]
-            normed[k] = work.tile([P, CB, hi - lo], F32, name="normed")
-            for cb in range(CB):
-                nc.vector.scalar_tensor_tensor(
-                    normed[k][:, cb, :], banks[k, cb][:], bias_c[cb], rstds[k][:], op0=ALU.add, op1=ALU.mult
+            first, end = chunks[k]
+            normed[k] = work.tile([P, end - first, C], F32, name="normed")
+            t_banks[k] = psum.tile([P, CB, end - first, NICHES], F32, name="t_bank", bufs=T_BANKS)
+            for node in range(first, end):
+                nc.vector.tensor_scalar_mul(
+                    normed[k][:, node - first, :], z_banks[k][:, node - first, :], rstd[:, node : node + 1]
                 )
+                for cb in range(CB):
+                    nc.tensor.transpose(
+                        t_banks[k][:, cb, node - first, :], normed[k][:, node - first, cb * P : (cb + 1) * P], identity[:]
+                    )
 
         def relu_part(k):
-            lo, hi = chunks[k]
-            relu_parts[k] = work.tile([P, CB, hi - lo], F32, name="relu_part")
+            first, end = chunks[k]
+            relu_parts[k] = work.tile([P, CB, end - first, NICHES], F32, name="relu_part")
             for cb in range(CB):
                 nc.scalar.activation(
-                    relu_parts[k][:, cb, :], normed[k][:, cb, :], ACT.Relu,
+                    relu_parts[k][:, cb], t_banks[k][:, cb], ACT.Relu,
                     bias=relu_scaled[:, cb, 1:2], scale=relu_scaled[:, cb, 0:1],
                 )
 
         def line_part(k):
-            lo, hi = chunks[k]
-            line_parts[k] = work.tile([P, CB, hi - lo], F32, name="line_part")
+            first, end = chunks[k]
+            line_parts[k] = work.tile([P, CB, end - first, NICHES], F32, name="line_part")
             for cb in range(CB):
                 nc.vector.scalar_tensor_tensor(
-                    line_parts[k][:, cb, :], normed[k][:, cb, :], line_scaled[:, cb, 0:1], h_beta[:, cb, lo:hi],
+                    line_parts[k][:, cb], t_banks[k][:, cb], line_scaled[:, cb, 0:1],
+                    h_beta[:, cb, first * NICHES : end * NICHES].rearrange("p (n q) -> p n q", q=NICHES),
                     op0=ALU.mult, op1=ALU.add,
                 )
 
         def add_and_store(k):
-            lo, hi = chunks[k]
-            result = work.tile([P, CB, hi - lo], F32, name="result")
-            nc.vector.tensor_add(result[:], line_parts[k][:], relu_parts[k][:])
-            nc.sync.dma_start(out.rearrange("(cb p) j -> p cb j", p=P)[:, :, lo:hi], result[:])
+            first, end = chunks[k]
+            result = work.tile([P, CB, end - first, NICHES], F32, name="result")
+            nc.gpsimd.tensor_add(result[:], line_parts[k][:], relu_parts[k][:])
+            nc.sync.dma_start(
+                out.rearrange("(cb p) j -> p cb j", p=P)[:, :, first * NICHES : end * NICHES],
+                result[:].rearrange("p cb n q -> p cb (n q)"),
+            )
 
         for kb in range(CB):
-            for i in range(n_pieces):
+            for i in range(len(pieces)):
                 look_up(kb, i)
         for kb in range(CB):
-            for k in range(CHUNKS_AHEAD):
+            for k in range(Z_BANKS):
                 project(k, kb)
-        nc.vector.tensor_copy(sum_bf[:], sum_term[:])
-        for k in range(CHUNKS_AHEAD):
+        nc.vector.tensor_add(sum_bf[:], sum_term[:], bias_rows[:])
+        for k in range(Z_BANKS):
             add_sum_term(k)
-        variance(0)
-        variance(1)
         reciprocal_std(0)
+        reciprocal_std(1)
+        normalise(0)
         for k in range(n_chunks):
-            normalise(k)
-            if k + CHUNKS_AHEAD < n_chunks:
-                for kb in range(CB):
-                    project(k + CHUNKS_AHEAD, kb)
-                add_sum_term(k + CHUNKS_AHEAD)
+            if k + 2 < n_chunks:
+                reciprocal_std(k + 2)
             if k + 1 < n_chunks:
-                reciprocal_std(k + 1)
+                normalise(k + 1)
+            if k + Z_BANKS < n_chunks:
+                for kb in range(CB):
+                    project(k + Z_BANKS, kb)
+                add_sum_term(k + Z_BANKS)
             relu_part(k)
             line_part(k)
-            if k + 2 < n_chunks:
-                variance(k + 2)
             add_and_store(k)

@@ -210,7 +210,8 @@ def tile_gnnnicheencoder_kernel(tc, x, w_l, w_r, b_l, gamma, beta, offs, out):
         def add_and_store(k):
             first, end = chunks[k]
             result = work.tile([P, CB, end - first, NICHES], F32, name="result")
-            nc.gpsimd.tensor_add(result[:], line_parts[k][:], relu_parts[k][:])
+            adder = nc.vector if k == n_chunks - 1 else nc.gpsimd
+            adder.tensor_add(result[:], line_parts[k][:], relu_parts[k][:])
             nc.sync.dma_start(
                 out.rearrange("(cb p) j -> p cb j", p=P)[:, :, first * NICHES : end * NICHES],
                 result[:].rearrange("p cb n q -> p cb (n q)"),

@@ -49,8 +49,8 @@ def tile_gnnnicheencoder_kernel(tc, x, w_l, w_r, b_l, gamma, beta, offs, out):
         nc.sync.dma_start(offsets[:], offs)
         store = [held.tile([P, S], F32, name=f"store{cb}") for cb in range(CB)]
         for cb in range(CB):
-            for half in range(2):
-                cells = slice(half * S // 2, (half + 1) * S // 2)
+            for quarter in range(4):
+                cells = slice(quarter * S // 4, (quarter + 1) * S // 4)
                 nc.sync.dma_start(store[cb][:, cells], x[cb * P : (cb + 1) * P, cells])
         wl_raw = held.tile([P, CB, C], BF16, name="wl_raw")
         wr_raw = held.tile([P, CB, C], BF16, name="wr_raw")

@@ -17,13 +17,14 @@ NICHES = 128
 N = NODES * NICHES
 LN_EPS = 1e-5
 LEAKY_SLOPE = 0.01
+TOP_WEIGHT = 99.0
+GAMMA_FLOOR = 1e-30
 
 FLOPS = 2 * 2 * C * C * N
 
 PIECE_NODES = (4, 4, 4, 4, 1)
 CHUNK_NODES = (1, 2, 2, 2, 2, 2, 2, 2, 2)
-Z_BANKS = 4
-T_BANKS = 3
+BANKS = 8
 
 
 def node_spans(node_counts):
@@ -42,7 +43,7 @@ def tile_gnnnicheencoder_kernel(tc, x, w_l, w_r, b_l, gamma, beta, offs, out):
     n_chunks = len(chunks)
     with (
         tc.tile_pool(name="held", bufs=1) as held,
-        tc.tile_pool(name="work", bufs=4) as work,
+        tc.tile_pool(name="work", bufs=n_chunks) as work,
         tc.psum_pool(name="psum", bufs=1) as psum,
     ):
         offsets = held.tile([P, N // 16], U16, name="offsets")
@@ -52,15 +53,20 @@ def tile_gnnnicheencoder_kernel(tc, x, w_l, w_r, b_l, gamma, beta, offs, out):
             for quarter in range(4):
                 cells = slice(quarter * S // 4, (quarter + 1) * S // 4)
                 nc.sync.dma_start(store[cb][:, cells], x[cb * P : (cb + 1) * P, cells])
+        gamma_row = held.tile([1, C], F32, name="gamma_row")
+        nc.scalar.dma_start(gamma_row[:], gamma.rearrange("c o -> o c"))
+        bias_row = held.tile([1, C], F32, name="bias_row")
+        nc.scalar.dma_start(bias_row[:], b_l.rearrange("c o -> o c"))
         wl_raw = held.tile([P, CB, C], BF16, name="wl_raw")
         wr_raw = held.tile([P, CB, C], BF16, name="wr_raw")
         nc.scalar.dma_start(wl_raw[:], w_l.rearrange("(kb p) c -> p kb c", p=P))
         nc.scalar.dma_start(wr_raw[:], w_r.rearrange("(kb p) c -> p kb c", p=P))
-        vectors = (b_l, gamma, beta)
-        rows = held.tile([P, C], F32, name="rows")
-        nc.vector.memset(rows[:], 0.0)
-        for r, vec in enumerate(vectors):
-            nc.scalar.dma_start(rows[r : r + 1, :], vec.rearrange("c o -> o c"))
+        gamma_rows = held.tile([P, C], F32, name="gamma_rows")
+        beta_rows = held.tile([P, C], F32, name="beta_rows")
+        for rows, vec in ((gamma_rows, gamma), (beta_rows, beta)):
+            nc.sync.dma_start(rows[:], vec.rearrange("c o -> (c o)").partition_broadcast(P))
+        gamma_columns = held.tile([P, CB], F32, name="gamma_columns")
+        nc.sync.dma_start(gamma_columns[:], gamma.rearrange("(cb p) o -> p (cb o)", p=P))
 
         eps = held.tile([P, 1], F32, name="eps")
         nc.vector.memset(eps[:], LN_EPS)
@@ -68,100 +74,123 @@ def tile_gnnnicheencoder_kernel(tc, x, w_l, w_r, b_l, gamma, beta, offs, out):
         make_identity(nc, identity[:])
         identity_bf = held.tile([P, P], BF16, name="identity_bf")
         nc.vector.tensor_copy(identity_bf[:], identity[:])
-        spread_row0 = held.tile([P, P], F32, name="spread_row0")
+        identity_99 = held.tile([P, P], BF16, name="identity_99")
+        nc.vector.tensor_scalar_mul(identity_99[:], identity[:], TOP_WEIGHT)
+        spread_row0 = held.tile([P, P], BF16, name="spread_row0")
         nc.vector.memset(spread_row0[:], 0.0)
         nc.vector.memset(spread_row0[0:1, :], 1.0)
         warm = held.tile([P, 1], F32, name="warm")
         nc.scalar.activation(warm[:], eps[:], ACT.Abs_reciprocal_sqrt)
 
+        sign_row = held.tile([P, C], BF16, name="sign_row")
+        nc.vector.memset(sign_row[:], 0.0)
+        nc.vector.tensor_scalar(sign_row[0:1, :], gamma_row[:], 0.0, 2.0, op0=ALU.is_ge, op1=ALU.mult)
+        nc.vector.tensor_scalar_add(sign_row[0:1, :], sign_row[0:1, :], -1.0)
+        sign_spread = psum.tile([P, C], F32, name="sign_spread", tag="bank0")
+        nc.tensor.matmul(sign_spread[:], spread_row0[:], sign_row[:], start=True, stop=True)
+        sign_rows = held.tile([P, C], F32, name="sign_rows")
+        nc.vector.tensor_copy(sign_rows[:], sign_spread[:])
         neg_bias_mean = held.tile([1, 1], F32, name="neg_bias_mean")
-        nc.vector.tensor_reduce(neg_bias_mean[:], rows[0:1, :], axis=AXIS_X, op=ALU.add)
+        nc.vector.tensor_reduce(neg_bias_mean[:], bias_row[:], axis=AXIS_X, op=ALU.add)
         nc.vector.tensor_scalar_mul(neg_bias_mean[:], neg_bias_mean[:], -1.0 / C)
-        nc.vector.tensor_scalar_add(rows[0:1, :], rows[0:1, :], neg_bias_mean[:])
-        bias_spread = psum.tile([P, C], F32, name="bias_spread", tag="sum_term")
-        nc.tensor.matmul(bias_spread[:], spread_row0[:], rows[:], start=True, stop=True)
-        bias_rows = held.tile([P, C], F32, name="bias_rows")
-        nc.vector.tensor_copy(bias_rows[:], bias_spread[:])
-        turned = psum.tile([P, CB, P], F32, name="turned", tag="sum_term")
-        for cb in range(CB):
-            nc.tensor.transpose(turned[:, cb, :], rows[:, cb * P : (cb + 1) * P], identity[:])
-        relu_scaled = held.tile([P, CB, 2], F32, name="relu_scaled")
-        nc.vector.tensor_scalar_mul(relu_scaled[:], turned[:, :, 1:3], 1.0 - LEAKY_SLOPE)
-        line_scaled = held.tile([P, CB, 2], F32, name="line_scaled")
-        nc.vector.tensor_scalar_mul(line_scaled[:], turned[:, :, 1:3], LEAKY_SLOPE)
+        bias_bf = held.tile([P, C], BF16, name="bias_bf")
+        nc.vector.memset(bias_bf[:], 0.0)
+        nc.vector.scalar_tensor_tensor(
+            bias_bf[0:1, :], bias_row[:], neg_bias_mean[:, 0:1], sign_rows[0:1, :], op0=ALU.add, op1=ALU.mult
+        )
 
         neg_mean = {}
         for raw, side in ((wl_raw, "l"), (wr_raw, "r")):
             neg_mean[side] = held.tile([P, CB], F32, name=f"neg_mean_{side}")
             nc.vector.tensor_reduce(neg_mean[side][:], raw[:], axis=AXIS_X, op=ALU.add)
             nc.vector.tensor_scalar_mul(neg_mean[side][:], neg_mean[side][:], -1.0 / C)
-        wl_16 = held.tile([P, CB, C], F32, name="wl_16")
+        wl_signed = held.tile([P, CB, C], F32, name="wl_signed")
+        wr_signed = held.tile([P, CB, C], F32, name="wr_signed")
         w_sum = held.tile([P, CB, C], BF16, name="w_sum")
         w_own = held.tile([P, CB, C], BF16, name="w_own")
         for kb in range(CB):
-            nc.vector.tensor_scalar(
-                wl_16[:, kb, :], wl_raw[:, kb, :], neg_mean["l"][:, kb : kb + 1], 1.0 / (NODES - 1),
-                op0=ALU.add, op1=ALU.mult,
-            )
-            nc.vector.tensor_copy(w_sum[:, kb, :], wl_16[:, kb, :])
+            for raw, side, signed in ((wl_raw, "l", wl_signed), (wr_raw, "r", wr_signed)):
+                nc.vector.scalar_tensor_tensor(
+                    signed[:, kb, :], raw[:, kb, :], neg_mean[side][:, kb : kb + 1], sign_rows[:],
+                    op0=ALU.add, op1=ALU.mult,
+                )
             nc.vector.scalar_tensor_tensor(
-                w_own[:, kb, :], wr_raw[:, kb, :], neg_mean["r"][:, kb : kb + 1], wl_16[:, kb, :],
-                op0=ALU.add, op1=ALU.subtract,
+                w_own[:, kb, :], wl_signed[:, kb, :], -1.0 / (NODES - 1), wr_signed[:, kb, :],
+                op0=ALU.mult, op1=ALU.add,
             )
+            nc.vector.tensor_scalar_mul(w_sum[:, kb, :], wl_signed[:, kb, :], 1.0 / (NODES - 1))
 
         h = held.tile([P, CB, N], F32, name="h")
         h_bf = held.tile([P, CB, N], BF16, name="h_bf")
-        h_beta = held.tile([P, CB, N], F32, name="h_beta")
-        sum_term = psum.tile([P, C], F32, name="sum_term")
-        sum_bf = held.tile([P, C], BF16, name="sum_bf")
+        h_sum = held.tile([P, CB, NICHES], F32, name="h_sum")
+        h_sum_bf = held.tile([P, CB, NICHES], BF16, name="h_sum_bf")
         square_sums = held.tile([P, NODES], F32, name="square_sums")
         rstd = held.tile([P, NODES], F32, name="rstd")
 
         def node_of(tile, kb, node):
             return tile[:, kb, node * NICHES : (node + 1) * NICHES]
 
-        def look_up(kb, i):
+        def chunk_of(tile, k):
+            first, end = chunks[k]
+            return tile[:, :, first * NICHES : end * NICHES].rearrange("p cb (n q) -> p cb n q", q=NICHES)
+
+        def columns_of(i):
             first, end = pieces[i]
-            lo, hi = first * NICHES, end * NICHES
-            nc.scalar.activation(h[:, kb, lo:hi], store[kb][:].indirect(offsets[:, lo // 16 : hi // 16]), ACT.Copy)
-            nc.vector.tensor_copy(h_bf[:, kb, lo:hi], h[:, kb, lo:hi])
-            for node in range(first, end):
-                nc.tensor.matmul(
-                    sum_term[:],
-                    node_of(h_bf, kb, node),
-                    w_sum[:, kb, :],
-                    start=(kb == 0 and node == 0),
-                    stop=(kb == CB - 1 and node == NODES - 1),
-                )
-            nc.vector.tensor_scalar_add(h_beta[:, kb, lo:hi], h[:, kb, lo:hi], line_scaled[:, kb, 1:2])
+            return slice(first * NICHES, end * NICHES)
+
+        def look_up(kb, i):
+            cols = columns_of(i)
+            nc.scalar.activation(
+                h[:, kb, cols], store[kb][:].indirect(offsets[:, cols.start // 16 : cols.stop // 16]), ACT.Copy
+            )
+
+        def round_h(kb, i):
+            cols = columns_of(i)
+            nc.vector.tensor_copy(h_bf[:, kb, cols], h[:, kb, cols])
+
+        def add_to_h_sum(kb, i):
+            piece = h[:, kb, columns_of(i)]
+            if i == len(pieces) - 1:
+                nc.vector.tensor_add(h_sum_bf[:, kb, :], h_sum[:, kb, :], piece)
+                return
+            by_niche = piece.rearrange("p (n q) -> p q n", q=NICHES)
+            if i == 0:
+                nc.vector.tensor_reduce(h_sum[:, kb, :], by_niche, axis=AXIS_X, op=ALU.add)
+            else:
+                part = work.tile([P, NICHES], F32, name="part")
+                nc.vector.tensor_reduce(part[:], by_niche, axis=AXIS_X, op=ALU.add)
+                nc.vector.tensor_add(h_sum[:, kb, :], h_sum[:, kb, :], part[:])
 
         z_banks = {}
-        normed = {}
-        t_banks = {}
-        relu_parts = {}
-        line_parts = {}
+        scaled = {}
+        turned_banks = {}
 
-        def project(k, kb):
+        def open_bank(k):
             first, end = chunks[k]
-            if kb == 0:
-                z_banks[k] = psum.tile([P, end - first, C], F32, name="z_bank", bufs=Z_BANKS)
-            for node in range(first, end):
+            z_banks[k] = psum.tile([P, end - first, C], F32, name="z_bank", tag=f"bank{k % BANKS}")
+            nc.tensor.matmul(
+                z_banks[k][:],
+                spread_row0[:],
+                bias_bf[:].unsqueeze(1).to_broadcast([P, end - first, C]),
+                start=True,
+                stop=False,
+            )
+
+        def project(k, kb, nodes):
+            first, end = chunks[k]
+            for node in range(max(first, nodes[0]), min(end, nodes[1])):
                 nc.tensor.matmul(
-                    z_banks[k][:, node - first, :],
-                    node_of(h_bf, kb, node),
-                    w_own[:, kb, :],
-                    start=(kb == 0 and node == first),
-                    stop=False,
+                    z_banks[k][:, node - first, :], node_of(h_bf, kb, node), w_own[:, kb, :], start=False, stop=False
                 )
 
-        def add_sum_term(k):
+        def add_sum_term(k, kb):
             first, end = chunks[k]
             nc.tensor.matmul(
                 z_banks[k][:],
-                identity_bf[:],
-                sum_bf[:].unsqueeze(1).to_broadcast([P, end - first, C]),
+                h_sum_bf[:, kb, :],
+                w_sum[:, kb, :].unsqueeze(1).to_broadcast([P, end - first, C]),
                 start=False,
-                stop=True,
+                stop=(kb == CB - 1),
             )
 
         def reciprocal_std(k):
@@ -175,69 +204,112 @@ def tile_gnnnicheencoder_kernel(tc, x, w_l, w_r, b_l, gamma, beta, offs, out):
                 rstd[:, first:end], square_sums[:, first:end], ACT.Abs_reciprocal_sqrt, bias=eps[:, 0:1], scale=1.0 / C
             )
 
-        def normalise(k):
+        def scale(k):
             first, end = chunks[k]
-            normed[k] = work.tile([P, end - first, C], F32, name="normed")
-            t_banks[k] = psum.tile([P, CB, end - first, NICHES], F32, name="t_bank", bufs=T_BANKS)
+            scaled[k] = work.tile([P, end - first, C], BF16, name="scaled")
             for node in range(first, end):
-                nc.vector.tensor_scalar_mul(
-                    normed[k][:, node - first, :], z_banks[k][:, node - first, :], rstd[:, node : node + 1]
-                )
-                for cb in range(CB):
-                    nc.tensor.transpose(
-                        t_banks[k][:, cb, node - first, :], normed[k][:, node - first, cb * P : (cb + 1) * P], identity[:]
-                    )
-
-        def relu_part(k):
-            first, end = chunks[k]
-            relu_parts[k] = work.tile([P, CB, end - first, NICHES], F32, name="relu_part")
-            for cb in range(CB):
-                nc.scalar.activation(
-                    relu_parts[k][:, cb], t_banks[k][:, cb], ACT.Relu,
-                    bias=relu_scaled[:, cb, 1:2], scale=relu_scaled[:, cb, 0:1],
-                )
-
-        def line_part(k):
-            first, end = chunks[k]
-            line_parts[k] = work.tile([P, CB, end - first, NICHES], F32, name="line_part")
-            for cb in range(CB):
                 nc.vector.scalar_tensor_tensor(
-                    line_parts[k][:, cb], t_banks[k][:, cb], line_scaled[:, cb, 0:1],
-                    h_beta[:, cb, first * NICHES : end * NICHES].rearrange("p (n q) -> p n q", q=NICHES),
+                    scaled[k][:, node - first, :], z_banks[k][:, node - first, :], rstd[:, node : node + 1], shift_rows[:],
                     op0=ALU.mult, op1=ALU.add,
                 )
 
-        def add_and_store(k):
+        def turn_back(k):
+            first, end = chunks[k]
+            top = work.tile([P, end - first, C], BF16, name="top")
+            nc.vector.tensor_scalar_max(top[:], scaled[k][:], 0.0)
+            turned_banks[k] = psum.tile([P, CB, end - first, NICHES], F32, name="turned_bank", tag=f"bank{k % BANKS}")
+            terms = [
+                (part, eye, node, cb)
+                for part, eye in ((scaled[k], identity_bf), (top, identity_99))
+                for node in range(end - first)
+                for cb in range(CB)
+            ]
+            for t, (part, eye, node, cb) in enumerate(terms):
+                nc.tensor.matmul(
+                    turned_banks[k][:, cb, node, :],
+                    part[:, node, cb * P : (cb + 1) * P],
+                    eye[:],
+                    start=(t == 0),
+                    stop=(t == len(terms) - 1),
+                )
+
+        def finish(k):
             first, end = chunks[k]
             result = work.tile([P, CB, end - first, NICHES], F32, name="result")
-            adder = nc.vector if k == n_chunks - 1 else nc.gpsimd
-            adder.tensor_add(result[:], line_parts[k][:], relu_parts[k][:])
+            if k % 2 == 0:
+                for cb in range(CB):
+                    nc.vector.scalar_tensor_tensor(
+                        result[:, cb], turned_banks[k][:, cb], out_scale[:, cb : cb + 1], chunk_of(h, k)[:, cb],
+                        op0=ALU.mult, op1=ALU.add,
+                    )
+            else:
+                leaky = work.tile([P, CB, end - first, NICHES], F32, name="leaky")
+                for cb in range(CB):
+                    nc.scalar.activation(leaky[:, cb], turned_banks[k][:, cb], ACT.Copy, scale=out_scale[:, cb : cb + 1])
+                nc.gpsimd.tensor_add(result[:], leaky[:], chunk_of(h, k))
             nc.sync.dma_start(
                 out.rearrange("(cb p) j -> p cb j", p=P)[:, :, first * NICHES : end * NICHES],
                 result[:].rearrange("p cb n q -> p cb (n q)"),
             )
 
-        for kb in range(CB):
-            for i in range(len(pieces)):
-                look_up(kb, i)
-        for kb in range(CB):
-            for k in range(Z_BANKS):
-                project(k, kb)
-        nc.vector.tensor_add(sum_bf[:], sum_term[:], bias_rows[:])
-        for k in range(Z_BANKS):
-            add_sum_term(k)
+        last = len(pieces) - 1
+        for k in range(BANKS):
+            open_bank(k)
+        for i in range(len(pieces)):
+            look_up(0, i)
+            round_h(0, i)
+            for k in range(BANKS):
+                project(k, 0, pieces[i])
+            add_to_h_sum(0, i)
+        for k in range(BANKS):
+            add_sum_term(k, 0)
+        for i in range(last - 1):
+            look_up(1, i)
+            round_h(1, i)
+            for k in range(BANKS):
+                project(k, 1, pieces[i])
+            add_to_h_sum(1, i)
+        for i in (last - 1, last):
+            look_up(1, i)
+            add_to_h_sum(1, i)
+        for k in range(3):
+            add_sum_term(k, 1)
+        for i in (last - 1, last):
+            round_h(1, i)
+            for k in range(BANKS):
+                project(k, 1, pieces[i])
+        gamma_abs = held.tile([P, C], F32, name="gamma_abs")
+        nc.vector.tensor_mul(gamma_abs[:], gamma_rows[:], sign_rows[:])
+        nc.vector.tensor_scalar_max(gamma_abs[:], gamma_abs[:], GAMMA_FLOOR)
+        shift_rows = held.tile([P, C], F32, name="shift_rows")
+        nc.vector.reciprocal(shift_rows[:], gamma_abs[:])
+        nc.vector.tensor_mul(shift_rows[:], shift_rows[:], beta_rows[:])
+        out_scale = held.tile([P, CB], F32, name="out_scale")
+        nc.vector.scalar_tensor_tensor(
+            out_scale[:], gamma_columns[:], -1.0, gamma_columns[:], op0=ALU.mult, op1=ALU.max
+        )
+        nc.vector.tensor_scalar(
+            out_scale[:], out_scale[:], GAMMA_FLOOR, LEAKY_SLOPE, op0=ALU.max, op1=ALU.mult
+        )
+
         reciprocal_std(0)
         reciprocal_std(1)
-        normalise(0)
-        for k in range(n_chunks):
-            if k + 2 < n_chunks:
-                reciprocal_std(k + 2)
-            if k + 1 < n_chunks:
-                normalise(k + 1)
-            if k + Z_BANKS < n_chunks:
+        scale(0)
+        turn_back(0)
+        for step in range(n_chunks + 1):
+            if step + 2 < n_chunks:
+                reciprocal_std(step + 2)
+            if step + 1 < n_chunks:
+                scale(step + 1)
+            if step >= 1:
+                finish(step - 1)
+            if step + 1 < n_chunks:
+                turn_back(step + 1)
+            if step + 3 < min(BANKS, n_chunks):
+                add_sum_term(step + 3, 1)
+            if step + BANKS - 1 < n_chunks and step >= 1:
+                late = step + BANKS - 1
+                open_bank(late)
                 for kb in range(CB):
-                    project(k + Z_BANKS, kb)
-                add_sum_term(k + Z_BANKS)
-            relu_part(k)
-            line_part(k)
-            add_and_store(k)
+                    project(late, kb, chunks[late])
+                    add_sum_term(late, kb)

@@ -22,8 +22,8 @@ GAMMA_FLOOR = 1e-30
 
 FLOPS = 2 * 2 * C * C * N
 
-PIECE_NODES = (4, 4, 4, 4, 1)
-CHUNK_NODES = (1, 2, 2, 2, 2, 2, 2, 2, 2)
+PIECE_NODES = ((4, 4, 4, 4, 1), (4, 4, 4, 2, 2, 1))
+CHUNK_NODES = (1, 2, 2, 2, 2, 2, 2, 2, 1, 1)
 BANKS = 8
 
 
@@ -38,7 +38,7 @@ def node_spans(node_counts):
 
 def tile_gnnnicheencoder_kernel(tc, x, w_l, w_r, b_l, gamma, beta, offs, out):
     nc = tc.nc
-    pieces = node_spans(PIECE_NODES)
+    pieces = [node_spans(node_counts) for node_counts in PIECE_NODES]
     chunks = node_spans(CHUNK_NODES)
     n_chunks = len(chunks)
     with (
@@ -53,20 +53,14 @@ def tile_gnnnicheencoder_kernel(tc, x, w_l, w_r, b_l, gamma, beta, offs, out):
             for quarter in range(4):
                 cells = slice(quarter * S // 4, (quarter + 1) * S // 4)
                 nc.sync.dma_start(store[cb][:, cells], x[cb * P : (cb + 1) * P, cells])
-        gamma_row = held.tile([1, C], F32, name="gamma_row")
-        nc.scalar.dma_start(gamma_row[:], gamma.rearrange("c o -> o c"))
-        bias_row = held.tile([1, C], F32, name="bias_row")
-        nc.scalar.dma_start(bias_row[:], b_l.rearrange("c o -> o c"))
+        vector_rows = {}
+        for name, vec in (("gamma", gamma), ("b_l", b_l), ("beta", beta)):
+            vector_rows[name] = held.tile([1, C], F32, name=f"{name}_row")
+            nc.scalar.dma_start(vector_rows[name][:], vec.rearrange("c o -> o c"))
         wl_raw = held.tile([P, CB, C], BF16, name="wl_raw")
         wr_raw = held.tile([P, CB, C], BF16, name="wr_raw")
         nc.scalar.dma_start(wl_raw[:], w_l.rearrange("(kb p) c -> p kb c", p=P))
         nc.scalar.dma_start(wr_raw[:], w_r.rearrange("(kb p) c -> p kb c", p=P))
-        gamma_rows = held.tile([P, C], F32, name="gamma_rows")
-        beta_rows = held.tile([P, C], F32, name="beta_rows")
-        for rows, vec in ((gamma_rows, gamma), (beta_rows, beta)):
-            nc.sync.dma_start(rows[:], vec.rearrange("c o -> (c o)").partition_broadcast(P))
-        gamma_columns = held.tile([P, CB], F32, name="gamma_columns")
-        nc.sync.dma_start(gamma_columns[:], gamma.rearrange("(cb p) o -> p (cb o)", p=P))
 
         eps = held.tile([P, 1], F32, name="eps")
         nc.vector.memset(eps[:], LN_EPS)
@@ -76,34 +70,36 @@ def tile_gnnnicheencoder_kernel(tc, x, w_l, w_r, b_l, gamma, beta, offs, out):
         nc.vector.tensor_copy(identity_bf[:], identity[:])
         identity_99 = held.tile([P, P], BF16, name="identity_99")
         nc.vector.tensor_scalar_mul(identity_99[:], identity[:], TOP_WEIGHT)
-        spread_row0 = held.tile([P, P], BF16, name="spread_row0")
-        nc.vector.memset(spread_row0[:], 0.0)
-        nc.vector.memset(spread_row0[0:1, :], 1.0)
+        ones = held.tile([1, P], F32, name="ones")
+        nc.vector.memset(ones[:], 1.0)
+        ones_bf = held.tile([1, P], BF16, name="ones_bf")
+        nc.vector.memset(ones_bf[:], 1.0)
         warm = held.tile([P, 1], F32, name="warm")
         nc.scalar.activation(warm[:], eps[:], ACT.Abs_reciprocal_sqrt)
 
-        sign_row = held.tile([P, C], BF16, name="sign_row")
-        nc.vector.memset(sign_row[:], 0.0)
-        nc.vector.tensor_scalar(sign_row[0:1, :], gamma_row[:], 0.0, 2.0, op0=ALU.is_ge, op1=ALU.mult)
-        nc.vector.tensor_scalar_add(sign_row[0:1, :], sign_row[0:1, :], -1.0)
+        sign_row = held.tile([1, C], BF16, name="sign_row")
+        nc.vector.tensor_scalar(sign_row[:], vector_rows["gamma"][:], 0.0, 2.0, op0=ALU.is_ge, op1=ALU.mult)
+        nc.vector.tensor_scalar_add(sign_row[:], sign_row[:], -1.0)
         sign_spread = psum.tile([P, C], F32, name="sign_spread", tag="bank0")
-        nc.tensor.matmul(sign_spread[:], spread_row0[:], sign_row[:], start=True, stop=True)
+        nc.tensor.matmul(sign_spread[:], ones_bf[:], sign_row[:], start=True, stop=True)
         sign_rows = held.tile([P, C], F32, name="sign_rows")
         nc.vector.tensor_copy(sign_rows[:], sign_spread[:])
         neg_bias_mean = held.tile([1, 1], F32, name="neg_bias_mean")
-        nc.vector.tensor_reduce(neg_bias_mean[:], bias_row[:], axis=AXIS_X, op=ALU.add)
+        nc.vector.tensor_reduce(neg_bias_mean[:], vector_rows["b_l"][:], axis=AXIS_X, op=ALU.add)
         nc.vector.tensor_scalar_mul(neg_bias_mean[:], neg_bias_mean[:], -1.0 / C)
-        bias_bf = held.tile([P, C], BF16, name="bias_bf")
-        nc.vector.memset(bias_bf[:], 0.0)
+        bias_bf = held.tile([1, C], BF16, name="bias_bf")
         nc.vector.scalar_tensor_tensor(
-            bias_bf[0:1, :], bias_row[:], neg_bias_mean[:, 0:1], sign_rows[0:1, :], op0=ALU.add, op1=ALU.mult
+            bias_bf[:], vector_rows["b_l"][:], neg_bias_mean[:], sign_row[:], op0=ALU.add, op1=ALU.mult
         )
 
         neg_mean = {}
         for raw, side in ((wl_raw, "l"), (wr_raw, "r")):
             neg_mean[side] = held.tile([P, CB], F32, name=f"neg_mean_{side}")
-            nc.vector.tensor_reduce(neg_mean[side][:], raw[:], axis=AXIS_X, op=ALU.add)
-            nc.vector.tensor_scalar_mul(neg_mean[side][:], neg_mean[side][:], -1.0 / C)
+            for kb in range(CB):
+                products = work.tile([P, C], BF16, name="products")
+                nc.scalar.activation(
+                    products[:], raw[:, kb, :], ACT.Copy, scale=-1.0 / C, accum_out=neg_mean[side][:, kb : kb + 1]
+                )
         wl_signed = held.tile([P, CB, C], F32, name="wl_signed")
         wr_signed = held.tile([P, CB, C], F32, name="wr_signed")
         w_sum = held.tile([P, CB, C], BF16, name="w_sum")
@@ -120,8 +116,44 @@ def tile_gnnnicheencoder_kernel(tc, x, w_l, w_r, b_l, gamma, beta, offs, out):
             )
             nc.vector.tensor_scalar_mul(w_sum[:, kb, :], wl_signed[:, kb, :], 1.0 / (NODES - 1))
 
+        turned_columns = psum.tile([P, 2, CB], F32, name="turned_columns", tag="bank1")
+        for v, name in enumerate(("gamma", "beta")):
+            for cb in range(CB):
+                nc.tensor.matmul(
+                    turned_columns[:, v, cb : cb + 1],
+                    vector_rows[name][:, cb * P : (cb + 1) * P],
+                    ones[:, 0:1],
+                    start=True,
+                    stop=True,
+                )
+        columns = held.tile([P, 2, CB], F32, name="columns")
+        nc.vector.tensor_copy(columns[:], turned_columns[:])
+        gamma_columns, beta_columns = columns[:, 0, :], columns[:, 1, :]
+        gamma_abs = held.tile([P, CB], F32, name="gamma_abs")
+        nc.vector.scalar_tensor_tensor(gamma_abs[:], gamma_columns, -1.0, gamma_columns, op0=ALU.mult, op1=ALU.max)
+        nc.vector.tensor_scalar_max(gamma_abs[:], gamma_abs[:], GAMMA_FLOOR)
+        out_scale = held.tile([P, CB], F32, name="out_scale")
+        nc.vector.tensor_scalar_mul(out_scale[:], gamma_abs[:], LEAKY_SLOPE)
+        floor_columns = held.tile([P, CB], F32, name="floor_columns")
+        nc.vector.reciprocal(floor_columns[:], gamma_abs[:])
+        nc.vector.scalar_tensor_tensor(
+            floor_columns[:], floor_columns[:], -1.0, beta_columns, op0=ALU.mult, op1=ALU.mult
+        )
+        floor_spread = psum.tile([P, C], F32, name="floor_spread", tag="bank2")
+        for cb in range(CB):
+            nc.tensor.matmul(
+                floor_spread[:, cb * P : (cb + 1) * P],
+                floor_columns[:, cb : cb + 1].to_broadcast([P, P]),
+                identity[:],
+                start=True,
+                stop=True,
+            )
+        floor_rows = held.tile([P, C], BF16, name="floor_rows")
+        nc.vector.tensor_copy(floor_rows[:], floor_spread[:])
+
         h = held.tile([P, CB, N], F32, name="h")
         h_bf = held.tile([P, CB, N], BF16, name="h_bf")
+        h_beta = held.tile([P, CB, N], F32, name="h_beta")
         h_sum = held.tile([P, CB, NICHES], F32, name="h_sum")
         h_sum_bf = held.tile([P, CB, NICHES], BF16, name="h_sum_bf")
         square_sums = held.tile([P, NODES], F32, name="square_sums")
@@ -134,63 +166,84 @@ def tile_gnnnicheencoder_kernel(tc, x, w_l, w_r, b_l, gamma, beta, offs, out):
             first, end = chunks[k]
             return tile[:, :, first * NICHES : end * NICHES].rearrange("p cb (n q) -> p cb n q", q=NICHES)
 
-        def columns_of(i):
-            first, end = pieces[i]
+        def columns_of(kb, i):
+            first, end = pieces[kb][i]
             return slice(first * NICHES, end * NICHES)
 
         def look_up(kb, i):
-            cols = columns_of(i)
+            cols = columns_of(kb, i)
             nc.scalar.activation(
                 h[:, kb, cols], store[kb][:].indirect(offsets[:, cols.start // 16 : cols.stop // 16]), ACT.Copy
             )
 
         def round_h(kb, i):
-            cols = columns_of(i)
+            cols = columns_of(kb, i)
             nc.vector.tensor_copy(h_bf[:, kb, cols], h[:, kb, cols])
 
-        def add_to_h_sum(kb, i):
-            piece = h[:, kb, columns_of(i)]
-            if i == len(pieces) - 1:
-                nc.vector.tensor_add(h_sum_bf[:, kb, :], h_sum[:, kb, :], piece)
-                return
-            by_niche = piece.rearrange("p (n q) -> p q n", q=NICHES)
-            if i == 0:
-                nc.vector.tensor_reduce(h_sum[:, kb, :], by_niche, axis=AXIS_X, op=ALU.add)
-            else:
-                part = work.tile([P, NICHES], F32, name="part")
-                nc.vector.tensor_reduce(part[:], by_niche, axis=AXIS_X, op=ALU.add)
-                nc.vector.tensor_add(h_sum[:, kb, :], h_sum[:, kb, :], part[:])
+        def add_beta(kb, nodes):
+            cols = slice(nodes[0] * NICHES, nodes[1] * NICHES)
+            nc.vector.tensor_scalar_add(h_beta[:, kb, cols], h[:, kb, cols], beta_columns[:, kb : kb + 1])
 
+        piece_sums = {}
+
+        def halve(kb, i):
+            nodes = piece_sums.get((kb, i), h[:, kb, columns_of(kb, i)])
+            width = nodes.shape[-1] // 2
+            half = work.tile([P, width], F32, name=f"half_{width}")
+            nc.vector.tensor_add(half[:], nodes[:, :width], nodes[:, width:])
+            piece_sums[kb, i] = half[:]
+
+        def add_to_h_sum(kb, i):
+            if i == 0:
+                return
+            so_far = piece_sums[kb, 0] if i == 1 else h_sum[:, kb, :]
+            if i == len(pieces[kb]) - 1:
+                nc.vector.tensor_add(h_sum_bf[:, kb, :], so_far, h[:, kb, columns_of(kb, i)])
+            else:
+                nc.vector.tensor_add(h_sum[:, kb, :], so_far, piece_sums[kb, i])
+
+        sum0_bf = held.tile([P, C], BF16, name="sum0_bf")
         z_banks = {}
         scaled = {}
         turned_banks = {}
 
-        def open_bank(k):
+        def add_own(k, kb, nodes):
             first, end = chunks[k]
-            z_banks[k] = psum.tile([P, end - first, C], F32, name="z_bank", tag=f"bank{k % BANKS}")
+            if kb == 0 and nodes[0] <= first < nodes[1]:
+                z_banks[k] = psum.tile([P, end - first, C], F32, name="z_bank", tag=f"bank{k % BANKS}")
+            for node in range(max(first, nodes[0]), min(end, nodes[1])):
+                nc.tensor.matmul(
+                    z_banks[k][:, node - first, :],
+                    node_of(h_bf, kb, node),
+                    w_own[:, kb, :],
+                    start=(kb == 0 and node == first),
+                    stop=False,
+                )
+
+        def make_sum0():
+            sum0 = psum.tile([P, C], F32, name="sum0", tag=f"bank{BANKS - 1}")
+            nc.tensor.matmul(sum0[:], ones_bf[:], bias_bf[:], start=True, stop=False)
+            nc.tensor.matmul(sum0[:], h_sum_bf[:, 0, :], w_sum[:, 0, :], start=False, stop=True)
+            nc.vector.tensor_copy(sum0_bf[:], sum0[:])
+
+        def add_sum0(k):
+            first, end = chunks[k]
             nc.tensor.matmul(
                 z_banks[k][:],
-                spread_row0[:],
-                bias_bf[:].unsqueeze(1).to_broadcast([P, end - first, C]),
-                start=True,
+                identity_bf[:],
+                sum0_bf[:].unsqueeze(1).to_broadcast([P, end - first, C]),
+                start=False,
                 stop=False,
             )
 
-        def project(k, kb, nodes):
-            first, end = chunks[k]
-            for node in range(max(first, nodes[0]), min(end, nodes[1])):
-                nc.tensor.matmul(
-                    z_banks[k][:, node - first, :], node_of(h_bf, kb, node), w_own[:, kb, :], start=False, stop=False
-                )
-
-        def add_sum_term(k, kb):
+        def add_sum1(k):
             first, end = chunks[k]
             nc.tensor.matmul(
                 z_banks[k][:],
-                h_sum_bf[:, kb, :],
-                w_sum[:, kb, :].unsqueeze(1).to_broadcast([P, end - first, C]),
+                h_sum_bf[:, 1, :],
+                w_sum[:, 1, :].unsqueeze(1).to_broadcast([P, end - first, C]),
                 start=False,
-                stop=(kb == CB - 1),
+                stop=True,
             )
 
         def reciprocal_std(k):
@@ -208,15 +261,18 @@ def tile_gnnnicheencoder_kernel(tc, x, w_l, w_r, b_l, gamma, beta, offs, out):
             first, end = chunks[k]
             scaled[k] = work.tile([P, end - first, C], BF16, name="scaled")
             for node in range(first, end):
-                nc.vector.scalar_tensor_tensor(
-                    scaled[k][:, node - first, :], z_banks[k][:, node - first, :], rstd[:, node : node + 1], shift_rows[:],
-                    op0=ALU.mult, op1=ALU.add,
-                )
+                t, z, factor = scaled[k][:, node - first, :], z_banks[k][:, node - first, :], rstd[:, node : node + 1]
+                if (n_chunks - 1 - k) % 3 == 0:
+                    nc.vector.tensor_scalar_mul(t, z, factor)
+                else:
+                    nc.scalar.activation(t, z, ACT.Copy, scale=factor)
 
         def turn_back(k):
             first, end = chunks[k]
             top = work.tile([P, end - first, C], BF16, name="top")
-            nc.vector.tensor_scalar_max(top[:], scaled[k][:], 0.0)
+            nc.vector.tensor_tensor(
+                top[:], scaled[k][:], floor_rows[:].unsqueeze(1).to_broadcast([P, end - first, C]), ALU.max
+            )
             turned_banks[k] = psum.tile([P, CB, end - first, NICHES], F32, name="turned_bank", tag=f"bank{k % BANKS}")
             terms = [
                 (part, eye, node, cb)
@@ -236,80 +292,77 @@ def tile_gnnnicheencoder_kernel(tc, x, w_l, w_r, b_l, gamma, beta, offs, out):
         def finish(k):
             first, end = chunks[k]
             result = work.tile([P, CB, end - first, NICHES], F32, name="result")
-            if k % 2 == 0:
-                for cb in range(CB):
-                    nc.vector.scalar_tensor_tensor(
-                        result[:, cb], turned_banks[k][:, cb], out_scale[:, cb : cb + 1], chunk_of(h, k)[:, cb],
-                        op0=ALU.mult, op1=ALU.add,
-                    )
-            else:
-                leaky = work.tile([P, CB, end - first, NICHES], F32, name="leaky")
-                for cb in range(CB):
-                    nc.scalar.activation(leaky[:, cb], turned_banks[k][:, cb], ACT.Copy, scale=out_scale[:, cb : cb + 1])
-                nc.gpsimd.tensor_add(result[:], leaky[:], chunk_of(h, k))
+            for cb in range(CB):
+                nc.vector.scalar_tensor_tensor(
+                    result[:, cb], turned_banks[k][:, cb], out_scale[:, cb : cb + 1], chunk_of(h_beta, k)[:, cb],
+                    op0=ALU.mult, op1=ALU.add,
+                )
             nc.sync.dma_start(
                 out.rearrange("(cb p) j -> p cb j", p=P)[:, :, first * NICHES : end * NICHES],
                 result[:].rearrange("p cb n q -> p cb (n q)"),
             )
 
-        last = len(pieces) - 1
-        for k in range(BANKS):
-            open_bank(k)
-        for i in range(len(pieces)):
+        early = range(BANKS - 1)
+        for i, span in enumerate(pieces[0]):
             look_up(0, i)
+            if i < len(pieces[0]) - 1:
+                halve(0, i)
+            if i > 0:
+                add_to_h_sum(0, i - 1)
             round_h(0, i)
-            for k in range(BANKS):
-                project(k, 0, pieces[i])
-            add_to_h_sum(0, i)
-        for k in range(BANKS):
-            add_sum_term(k, 0)
-        for i in range(last - 1):
+            if i < len(pieces[0]) - 1:
+                halve(0, i)
+            for k in early:
+                add_own(k, 0, span)
+            add_beta(0, span)
+        add_to_h_sum(0, len(pieces[0]) - 1)
+        make_sum0()
+        for k in early:
+            add_sum0(k)
+        add_own(BANKS - 1, 0, chunks[BANKS - 1])
+        add_sum0(BANKS - 1)
+        short = [i for i, (first, end) in enumerate(pieces[1]) if end - first < 4]
+        for i in range(short[0]):
             look_up(1, i)
+            halve(1, i)
+            if i > 0:
+                add_to_h_sum(1, i - 1)
             round_h(1, i)
+            halve(1, i)
             for k in range(BANKS):
-                project(k, 1, pieces[i])
-            add_to_h_sum(1, i)
-        for i in (last - 1, last):
+                add_own(k, 1, pieces[1][i])
+        for i in short:
             look_up(1, i)
-            add_to_h_sum(1, i)
+            if i != short[-1]:
+                halve(1, i)
+            add_to_h_sum(1, i - 1)
+        add_to_h_sum(1, short[-1])
         for k in range(3):
-            add_sum_term(k, 1)
-        for i in (last - 1, last):
+            add_sum1(k)
+        for i in short:
             round_h(1, i)
             for k in range(BANKS):
-                project(k, 1, pieces[i])
-        gamma_abs = held.tile([P, C], F32, name="gamma_abs")
-        nc.vector.tensor_mul(gamma_abs[:], gamma_rows[:], sign_rows[:])
-        nc.vector.tensor_scalar_max(gamma_abs[:], gamma_abs[:], GAMMA_FLOOR)
-        shift_rows = held.tile([P, C], F32, name="shift_rows")
-        nc.vector.reciprocal(shift_rows[:], gamma_abs[:])
-        nc.vector.tensor_mul(shift_rows[:], shift_rows[:], beta_rows[:])
-        out_scale = held.tile([P, CB], F32, name="out_scale")
-        nc.vector.scalar_tensor_tensor(
-            out_scale[:], gamma_columns[:], -1.0, gamma_columns[:], op0=ALU.mult, op1=ALU.max
-        )
-        nc.vector.tensor_scalar(
-            out_scale[:], out_scale[:], GAMMA_FLOOR, LEAKY_SLOPE, op0=ALU.max, op1=ALU.mult
-        )
+                add_own(k, 1, pieces[1][i])
+        for span in pieces[0]:
+            add_beta(1, span)
 
         reciprocal_std(0)
         reciprocal_std(1)
         scale(0)
-        turn_back(0)
-        for step in range(n_chunks + 1):
+        for step in range(n_chunks + 2):
             if step + 2 < n_chunks:
                 reciprocal_std(step + 2)
             if step + 1 < n_chunks:
                 scale(step + 1)
-            if step >= 1:
-                finish(step - 1)
-            if step + 1 < n_chunks:
-                turn_back(step + 1)
+            if step < n_chunks:
+                turn_back(step)
+            if step >= 2:
+                finish(step - 2)
             if step + 3 < min(BANKS, n_chunks):
-                add_sum_term(step + 3, 1)
-            if step + BANKS - 1 < n_chunks and step >= 1:
-                late = step + BANKS - 1
-                open_bank(late)
+                add_sum1(step + 3)
+            if step >= 2 and step + BANKS - 2 < n_chunks:
+                late = step + BANKS - 2
                 for kb in range(CB):
-                    project(late, kb, chunks[late])
-                    add_sum_term(late, kb)
+                    add_own(late, kb, chunks[late])
+                add_sum0(late)
+                add_sum1(late)

@@ -23,8 +23,11 @@ GAMMA_FLOOR = 1e-30
 FLOPS = 2 * 2 * C * C * N
 
 PIECE_NODES = ((4, 4, 4, 4, 1), (4, 4, 4, 2, 2, 1))
-CHUNK_NODES = (1, 2, 2, 2, 2, 2, 2, 2, 1, 1)
+VECTOR_CHUNKS = ((0, 1), (9, 11), (11, 13), (13, 15), (15, 17))
+SCALAR_CHUNKS = ((1, 3), (3, 5), (5, 7), (7, 8), (8, 9))
+CHUNKS = VECTOR_CHUNKS + SCALAR_CHUNKS
 BANKS = 8
+SUM_AHEAD = 5
 
 
 def node_spans(node_counts):
@@ -39,8 +42,9 @@ def node_spans(node_counts):
 def tile_gnnnicheencoder_kernel(tc, x, w_l, w_r, b_l, gamma, beta, offs, out):
     nc = tc.nc
     pieces = [node_spans(node_counts) for node_counts in PIECE_NODES]
-    chunks = node_spans(CHUNK_NODES)
+    chunks = CHUNKS
     n_chunks = len(chunks)
+    scalar_nodes = (SCALAR_CHUNKS[0][0], SCALAR_CHUNKS[-1][1])
     with (
         tc.tile_pool(name="held", bufs=1) as held,
         tc.tile_pool(name="work", bufs=n_chunks) as work,
@@ -80,7 +84,7 @@ def tile_gnnnicheencoder_kernel(tc, x, w_l, w_r, b_l, gamma, beta, offs, out):
         sign_row = held.tile([1, C], BF16, name="sign_row")
         nc.vector.tensor_scalar(sign_row[:], vector_rows["gamma"][:], 0.0, 2.0, op0=ALU.is_ge, op1=ALU.mult)
         nc.vector.tensor_scalar_add(sign_row[:], sign_row[:], -1.0)
-        sign_spread = psum.tile([P, C], F32, name="sign_spread", tag="bank0")
+        sign_spread = psum.tile([P, C], F32, name="sign_spread", tag="bank4")
         nc.tensor.matmul(sign_spread[:], ones_bf[:], sign_row[:], start=True, stop=True)
         sign_rows = held.tile([P, C], F32, name="sign_rows")
         nc.vector.tensor_copy(sign_rows[:], sign_spread[:])
@@ -116,7 +120,7 @@ def tile_gnnnicheencoder_kernel(tc, x, w_l, w_r, b_l, gamma, beta, offs, out):
             )
             nc.vector.tensor_scalar_mul(w_sum[:, kb, :], wl_signed[:, kb, :], 1.0 / (NODES - 1))
 
-        turned_columns = psum.tile([P, 2, CB], F32, name="turned_columns", tag="bank1")
+        turned_columns = psum.tile([P, 2, CB], F32, name="turned_columns", tag="bank5")
         for v, name in enumerate(("gamma", "beta")):
             for cb in range(CB):
                 nc.tensor.matmul(
@@ -134,28 +138,28 @@ def tile_gnnnicheencoder_kernel(tc, x, w_l, w_r, b_l, gamma, beta, offs, out):
         nc.vector.tensor_scalar_max(gamma_abs[:], gamma_abs[:], GAMMA_FLOOR)
         out_scale = held.tile([P, CB], F32, name="out_scale")
         nc.vector.tensor_scalar_mul(out_scale[:], gamma_abs[:], LEAKY_SLOPE)
-        floor_columns = held.tile([P, CB], F32, name="floor_columns")
-        nc.vector.reciprocal(floor_columns[:], gamma_abs[:])
-        nc.vector.scalar_tensor_tensor(
-            floor_columns[:], floor_columns[:], -1.0, beta_columns, op0=ALU.mult, op1=ALU.mult
-        )
-        floor_spread = psum.tile([P, C], F32, name="floor_spread", tag="bank2")
+        shift_columns = held.tile([P, CB], F32, name="shift_columns")
+        nc.vector.reciprocal(shift_columns[:], gamma_abs[:])
+        nc.vector.tensor_mul(shift_columns[:], shift_columns[:], beta_columns)
+        shift_spread = psum.tile([P, C], F32, name="shift_spread", tag="bank6")
         for cb in range(CB):
             nc.tensor.matmul(
-                floor_spread[:, cb * P : (cb + 1) * P],
-                floor_columns[:, cb : cb + 1].to_broadcast([P, P]),
+                shift_spread[:, cb * P : (cb + 1) * P],
+                shift_columns[:, cb : cb + 1].to_broadcast([P, P]),
                 identity[:],
                 start=True,
                 stop=True,
             )
+        shift_rows = held.tile([P, C], F32, name="shift_rows")
+        nc.vector.tensor_copy(shift_rows[:], shift_spread[:])
         floor_rows = held.tile([P, C], BF16, name="floor_rows")
-        nc.vector.tensor_copy(floor_rows[:], floor_spread[:])
+        nc.vector.tensor_scalar_mul(floor_rows[:], shift_spread[:], -1.0)
 
         h = held.tile([P, CB, N], F32, name="h")
         h_bf = held.tile([P, CB, N], BF16, name="h_bf")
         h_beta = held.tile([P, CB, N], F32, name="h_beta")
-        h_sum = held.tile([P, CB, NICHES], F32, name="h_sum")
-        h_sum_bf = held.tile([P, CB, NICHES], BF16, name="h_sum_bf")
+        h_sum = held.tile([P, NICHES], F32, name="h_sum")
+        h_sum_bf = held.tile([P, NICHES], BF16, name="h_sum_bf")
         square_sums = held.tile([P, NODES], F32, name="square_sums")
         rstd = held.tile([P, NODES], F32, name="rstd")
 
@@ -180,28 +184,41 @@ def tile_gnnnicheencoder_kernel(tc, x, w_l, w_r, b_l, gamma, beta, offs, out):
             cols = columns_of(kb, i)
             nc.vector.tensor_copy(h_bf[:, kb, cols], h[:, kb, cols])
 
-        def add_beta(kb, nodes):
-            cols = slice(nodes[0] * NICHES, nodes[1] * NICHES)
-            nc.vector.tensor_scalar_add(h_beta[:, kb, cols], h[:, kb, cols], beta_columns[:, kb : kb + 1])
+        def scalar_columns(span):
+            return slice(max(span[0], scalar_nodes[0]) * NICHES, min(span[1], scalar_nodes[1]) * NICHES)
+
+        def add_beta(kb, span):
+            cols = scalar_columns(span)
+            if cols.start < cols.stop:
+                nc.vector.tensor_scalar_add(h_beta[:, kb, cols], h[:, kb, cols], beta_columns[:, kb : kb + 1])
 
         piece_sums = {}
 
-        def halve(kb, i):
-            nodes = piece_sums.get((kb, i), h[:, kb, columns_of(kb, i)])
+        def halve(i):
+            nodes = piece_sums.get(i, h[:, 1, columns_of(1, i)])
             width = nodes.shape[-1] // 2
             half = work.tile([P, width], F32, name=f"half_{width}")
             nc.vector.tensor_add(half[:], nodes[:, :width], nodes[:, width:])
-            piece_sums[kb, i] = half[:]
+            piece_sums[i] = half[:]
 
-        def add_to_h_sum(kb, i):
-            if i == 0:
+        def add_to_h_sum(i):
+            if i == 1:
                 return
-            so_far = piece_sums[kb, 0] if i == 1 else h_sum[:, kb, :]
-            if i == len(pieces[kb]) - 1:
-                nc.vector.tensor_add(h_sum_bf[:, kb, :], so_far, h[:, kb, columns_of(kb, i)])
+            so_far = piece_sums[1] if i == 2 else h_sum[:]
+            if i == len(pieces[1]) - 1:
+                nc.vector.tensor_add(h_sum_bf[:], so_far, h[:, 1, columns_of(1, i)])
             else:
-                nc.vector.tensor_add(h_sum[:, kb, :], so_far, piece_sums[kb, i])
+                nc.vector.tensor_add(h_sum[:], so_far, piece_sums[i])
 
+        def add_to_sum0(kb, i):
+            if kb == 0 and i == 0:
+                nc.tensor.matmul(sum0[:], ones_bf[:], bias_bf[:], start=True, stop=False)
+            for node in range(*pieces[kb][i]):
+                closes = kb == 1 and node == pieces[1][0][1] - 1
+                nc.tensor.matmul(sum0[:], node_of(h_bf, kb, node), w_sum[:, kb, :], start=False, stop=closes)
+
+        SUM_BANK = f"bank{BANKS - 1}"
+        sum0 = psum.tile([P, C], F32, name="sum0", tag=SUM_BANK)
         sum0_bf = held.tile([P, C], BF16, name="sum0_bf")
         z_banks = {}
         scaled = {}
@@ -220,12 +237,6 @@ def tile_gnnnicheencoder_kernel(tc, x, w_l, w_r, b_l, gamma, beta, offs, out):
                     stop=False,
                 )
 
-        def make_sum0():
-            sum0 = psum.tile([P, C], F32, name="sum0", tag=f"bank{BANKS - 1}")
-            nc.tensor.matmul(sum0[:], ones_bf[:], bias_bf[:], start=True, stop=False)
-            nc.tensor.matmul(sum0[:], h_sum_bf[:, 0, :], w_sum[:, 0, :], start=False, stop=True)
-            nc.vector.tensor_copy(sum0_bf[:], sum0[:])
-
         def add_sum0(k):
             first, end = chunks[k]
             nc.tensor.matmul(
@@ -240,7 +251,7 @@ def tile_gnnnicheencoder_kernel(tc, x, w_l, w_r, b_l, gamma, beta, offs, out):
             first, end = chunks[k]
             nc.tensor.matmul(
                 z_banks[k][:],
-                h_sum_bf[:, 1, :],
+                h_sum_bf[:],
                 w_sum[:, 1, :].unsqueeze(1).to_broadcast([P, end - first, C]),
                 start=False,
                 stop=True,
@@ -257,22 +268,28 @@ def tile_gnnnicheencoder_kernel(tc, x, w_l, w_r, b_l, gamma, beta, offs, out):
                 rstd[:, first:end], square_sums[:, first:end], ACT.Abs_reciprocal_sqrt, bias=eps[:, 0:1], scale=1.0 / C
             )
 
+        def by_scalar(k):
+            return k >= len(VECTOR_CHUNKS)
+
         def scale(k):
             first, end = chunks[k]
             scaled[k] = work.tile([P, end - first, C], BF16, name="scaled")
             for node in range(first, end):
-                t, z, factor = scaled[k][:, node - first, :], z_banks[k][:, node - first, :], rstd[:, node : node + 1]
-                if (n_chunks - 1 - k) % 3 == 0:
-                    nc.vector.tensor_scalar_mul(t, z, factor)
+                to, z, factor = scaled[k][:, node - first, :], z_banks[k][:, node - first, :], rstd[:, node : node + 1]
+                if by_scalar(k):
+                    nc.scalar.activation(to, z, ACT.Copy, scale=factor)
                 else:
-                    nc.scalar.activation(t, z, ACT.Copy, scale=factor)
+                    nc.vector.scalar_tensor_tensor(to, z, factor, shift_rows[:], op0=ALU.mult, op1=ALU.add)
 
         def turn_back(k):
             first, end = chunks[k]
             top = work.tile([P, end - first, C], BF16, name="top")
-            nc.vector.tensor_tensor(
-                top[:], scaled[k][:], floor_rows[:].unsqueeze(1).to_broadcast([P, end - first, C]), ALU.max
-            )
+            if by_scalar(k):
+                nc.vector.tensor_tensor(
+                    top[:], scaled[k][:], floor_rows[:].unsqueeze(1).to_broadcast([P, end - first, C]), ALU.max
+                )
+            else:
+                nc.vector.tensor_scalar_max(top[:], scaled[k][:], 0.0)
             turned_banks[k] = psum.tile([P, CB, end - first, NICHES], F32, name="turned_bank", tag=f"bank{k % BANKS}")
             terms = [
                 (part, eye, node, cb)
@@ -291,10 +308,11 @@ def tile_gnnnicheencoder_kernel(tc, x, w_l, w_r, b_l, gamma, beta, offs, out):
 
         def finish(k):
             first, end = chunks[k]
+            residual = chunk_of(h_beta if by_scalar(k) else h, k)
             result = work.tile([P, CB, end - first, NICHES], F32, name="result")
             for cb in range(CB):
                 nc.vector.scalar_tensor_tensor(
-                    result[:, cb], turned_banks[k][:, cb], out_scale[:, cb : cb + 1], chunk_of(h_beta, k)[:, cb],
+                    result[:, cb], turned_banks[k][:, cb], out_scale[:, cb : cb + 1], residual[:, cb],
                     op0=ALU.mult, op1=ALU.add,
                 )
             nc.sync.dma_start(
@@ -305,46 +323,49 @@ def tile_gnnnicheencoder_kernel(tc, x, w_l, w_r, b_l, gamma, beta, offs, out):
         early = range(BANKS - 1)
         for i, span in enumerate(pieces[0]):
             look_up(0, i)
-            if i < len(pieces[0]) - 1:
-                halve(0, i)
-            if i > 0:
-                add_to_h_sum(0, i - 1)
             round_h(0, i)
-            if i < len(pieces[0]) - 1:
-                halve(0, i)
+            add_to_sum0(0, i)
             for k in early:
                 add_own(k, 0, span)
             add_beta(0, span)
-        add_to_h_sum(0, len(pieces[0]) - 1)
-        make_sum0()
-        for k in early:
-            add_sum0(k)
-        add_own(BANKS - 1, 0, chunks[BANKS - 1])
-        add_sum0(BANKS - 1)
         short = [i for i, (first, end) in enumerate(pieces[1]) if end - first < 4]
         for i in range(short[0]):
             look_up(1, i)
-            halve(1, i)
             if i > 0:
-                add_to_h_sum(1, i - 1)
+                halve(i)
+            if i > 1:
+                add_to_h_sum(i - 1)
             round_h(1, i)
-            halve(1, i)
-            for k in range(BANKS):
+            if i > 0:
+                halve(i)
+            for k in early:
                 add_own(k, 1, pieces[1][i])
+            if i == 0:
+                add_to_sum0(1, i)
+                add_beta(1, pieces[1][i])
+            if i == 1:
+                nc.vector.tensor_copy(sum0_bf[:], sum0[:])
+        for k in early:
+            add_sum0(k)
         for i in short:
             look_up(1, i)
             if i != short[-1]:
-                halve(1, i)
-            add_to_h_sum(1, i - 1)
-        add_to_h_sum(1, short[-1])
-        for k in range(3):
+                halve(i)
+            add_to_h_sum(i - 1)
+        add_to_h_sum(short[-1])
+        gathered = [k for k in range(SUM_AHEAD) if chunks[k][1] <= pieces[1][short[0]][0]]
+        for k in gathered:
             add_sum1(k)
+        short_cols = slice(pieces[1][short[0]][0] * NICHES, N)
+        nc.scalar.copy(h_bf[:, 1, short_cols], h[:, 1, short_cols])
         for i in short:
-            round_h(1, i)
-            for k in range(BANKS):
+            for k in early:
                 add_own(k, 1, pieces[1][i])
-        for span in pieces[0]:
-            add_beta(1, span)
+        for k in range(SUM_AHEAD):
+            if k not in gathered:
+                add_sum1(k)
+        cols = scalar_columns((pieces[1][0][1], NODES))
+        nc.scalar.activation(h_beta[:, 1, cols], h[:, 1, cols], ACT.Identity, bias=beta_columns[:, 1:2])
 
         reciprocal_std(0)
         reciprocal_std(1)
@@ -358,11 +379,11 @@ def tile_gnnnicheencoder_kernel(tc, x, w_l, w_r, b_l, gamma, beta, offs, out):
                 turn_back(step)
             if step >= 2:
                 finish(step - 2)
-            if step + 3 < min(BANKS, n_chunks):
-                add_sum1(step + 3)
-            if step >= 2 and step + BANKS - 2 < n_chunks:
-                late = step + BANKS - 2
-                for kb in range(CB):
-                    add_own(late, kb, chunks[late])
-                add_sum0(late)
-                add_sum1(late)
+            if step + SUM_AHEAD < BANKS - 1:
+                add_sum1(step + SUM_AHEAD)
+            for k in range(BANKS - 1, n_chunks):
+                if step == max(0, k - BANKS + 2):
+                    for kb in range(CB):
+                        add_own(k, kb, chunks[k])
+                    add_sum0(k)
+                    add_sum1(k)

@@ -152,8 +152,8 @@ def tile_gnnnicheencoder_kernel(tc, x, w_l, w_r, b_l, gamma, beta, offs, out):
             )
         shift_rows = held.tile([P, C], F32, name="shift_rows")
         nc.vector.tensor_copy(shift_rows[:], shift_spread[:])
-        floor_rows = held.tile([P, C], BF16, name="floor_rows")
-        nc.vector.tensor_scalar_mul(floor_rows[:], shift_spread[:], -1.0)
+        floor_rows = held.tile([P, 2, C], BF16, name="floor_rows")
+        nc.vector.tensor_scalar_mul(floor_rows[:], shift_spread[:].unsqueeze(1).to_broadcast([P, 2, C]), -1.0)
 
         h = held.tile([P, CB, N], F32, name="h")
         h_bf = held.tile([P, CB, N], BF16, name="h_bf")
@@ -205,10 +205,13 @@ def tile_gnnnicheencoder_kernel(tc, x, w_l, w_r, b_l, gamma, beta, offs, out):
             if i == 1:
                 return
             so_far = piece_sums[1] if i == 2 else h_sum[:]
-            if i == len(pieces[1]) - 1:
-                nc.vector.tensor_add(h_sum_bf[:], so_far, h[:, 1, columns_of(1, i)])
-            else:
-                nc.vector.tensor_add(h_sum[:], so_far, piece_sums[i])
+            nc.vector.tensor_add(h_sum[:], so_far, piece_sums[i])
+
+        def close_h_sum():
+            last = len(pieces[1]) - 1
+            last_two = work.tile([P, NICHES], F32, name="last_two")
+            nc.vector.tensor_add(last_two[:], piece_sums[last - 1], h[:, 1, columns_of(1, last)])
+            nc.vector.tensor_add(h_sum_bf[:], h_sum[:], last_two[:])
 
         def add_to_sum0(kb, i):
             if kb == 0 and i == 0:
@@ -285,9 +288,7 @@ def tile_gnnnicheencoder_kernel(tc, x, w_l, w_r, b_l, gamma, beta, offs, out):
             first, end = chunks[k]
             top = work.tile([P, end - first, C], BF16, name="top")
             if by_scalar(k):
-                nc.vector.tensor_tensor(
-                    top[:], scaled[k][:], floor_rows[:].unsqueeze(1).to_broadcast([P, end - first, C]), ALU.max
-                )
+                nc.vector.tensor_tensor(top[:], scaled[k][:], floor_rows[:, : end - first, :], ALU.max)
             else:
                 nc.vector.tensor_scalar_max(top[:], scaled[k][:], 0.0)
             turned_banks[k] = psum.tile([P, CB, end - first, NICHES], F32, name="turned_bank", tag=f"bank{k % BANKS}")
@@ -351,8 +352,8 @@ def tile_gnnnicheencoder_kernel(tc, x, w_l, w_r, b_l, gamma, beta, offs, out):
             look_up(1, i)
             if i != short[-1]:
                 halve(i)
-            add_to_h_sum(i - 1)
-        add_to_h_sum(short[-1])
+                add_to_h_sum(i - 1)
+        close_h_sum()
         gathered = [k for k in range(SUM_AHEAD) if chunks[k][1] <= pieces[1][short[0]][0]]
         for k in gathered:
             add_sum1(k)

@@ -22,7 +22,7 @@ GAMMA_FLOOR = 1e-30
 
 FLOPS = 2 * 2 * C * C * N
 
-PIECE_NODES = ((4, 4, 4, 4, 1), (4, 4, 4, 2, 2, 1))
+PIECE_NODES = ((4, 4, 4, 5), (4, 4, 4, 2, 2, 1))
 VECTOR_CHUNKS = ((0, 1), (9, 11), (11, 13), (13, 15), (15, 17))
 SCALAR_CHUNKS = ((1, 3), (3, 5), (5, 7), (7, 8), (8, 9))
 CHUNKS = VECTOR_CHUNKS + SCALAR_CHUNKS
@@ -346,6 +346,8 @@ def tile_gnnnicheencoder_kernel(tc, x, w_l, w_r, b_l, gamma, beta, offs, out):
                 add_beta(1, pieces[1][i])
             if i == 1:
                 nc.vector.tensor_copy(sum0_bf[:], sum0[:])
+            if i == 2:
+                add_beta(1, (pieces[1][1][0], pieces[1][2][1]))
         for k in early:
             add_sum0(k)
         for i in short:
@@ -365,8 +367,6 @@ def tile_gnnnicheencoder_kernel(tc, x, w_l, w_r, b_l, gamma, beta, offs, out):
         for k in range(SUM_AHEAD):
             if k not in gathered:
                 add_sum1(k)
-        cols = scalar_columns((pieces[1][0][1], NODES))
-        nc.scalar.activation(h_beta[:, 1, cols], h[:, 1, cols], ACT.Identity, bias=beta_columns[:, 1:2])
 
         reciprocal_std(0)
         reciprocal_std(1)

@@ -99,11 +99,8 @@ def tile_gnnnicheencoder_kernel(tc, x, w_l, w_r, b_l, gamma, beta, offs, out):
         neg_mean = {}
         for raw, side in ((wl_raw, "l"), (wr_raw, "r")):
             neg_mean[side] = held.tile([P, CB], F32, name=f"neg_mean_{side}")
-            for kb in range(CB):
-                products = work.tile([P, C], BF16, name="products")
-                nc.scalar.activation(
-                    products[:], raw[:, kb, :], ACT.Copy, scale=-1.0 / C, accum_out=neg_mean[side][:, kb : kb + 1]
-                )
+            nc.vector.tensor_reduce(neg_mean[side][:], raw[:], axis=AXIS_X, op=ALU.add)
+            nc.vector.tensor_scalar_mul(neg_mean[side][:], neg_mean[side][:], -1.0 / C)
         wl_signed = held.tile([P, CB, C], F32, name="wl_signed")
         wr_signed = held.tile([P, CB, C], F32, name="wr_signed")
         w_sum = held.tile([P, CB, C], BF16, name="w_sum")

@@ -23,8 +23,8 @@ GAMMA_FLOOR = 1e-30
 FLOPS = 2 * 2 * C * C * N
 
 PIECE_NODES = ((4, 4, 4, 5), (4, 4, 4, 2, 2, 1))
-VECTOR_CHUNKS = ((0, 1), (9, 11), (11, 13), (13, 15), (15, 17))
-SCALAR_CHUNKS = ((1, 3), (3, 5), (5, 7), (7, 8), (8, 9))
+VECTOR_CHUNKS = ((0, 1), (1, 3), (3, 5), (5, 7), (7, 9))
+SCALAR_CHUNKS = ((9, 11), (11, 13), (13, 15), (15, 16), (16, 17))
 CHUNKS = VECTOR_CHUNKS + SCALAR_CHUNKS
 BANKS = 8
 SUM_AHEAD = 5
@@ -340,11 +340,8 @@ def tile_gnnnicheencoder_kernel(tc, x, w_l, w_r, b_l, gamma, beta, offs, out):
                 add_own(k, 1, pieces[1][i])
             if i == 0:
                 add_to_sum0(1, i)
-                add_beta(1, pieces[1][i])
             if i == 1:
                 nc.vector.tensor_copy(sum0_bf[:], sum0[:])
-            if i == 2:
-                add_beta(1, (pieces[1][1][0], pieces[1][2][1]))
         for k in early:
             add_sum0(k)
         for i in short:
@@ -353,17 +350,16 @@ def tile_gnnnicheencoder_kernel(tc, x, w_l, w_r, b_l, gamma, beta, offs, out):
                 halve(i)
                 add_to_h_sum(i - 1)
         close_h_sum()
-        gathered = [k for k in range(SUM_AHEAD) if chunks[k][1] <= pieces[1][short[0]][0]]
-        for k in gathered:
+        for k in range(SUM_AHEAD):
             add_sum1(k)
-        short_cols = slice(pieces[1][short[0]][0] * NICHES, N)
+        first_short = pieces[1][short[0]][0]
+        short_cols = slice(first_short * NICHES, N)
         nc.scalar.copy(h_bf[:, 1, short_cols], h[:, 1, short_cols])
         for i in short:
             for k in early:
                 add_own(k, 1, pieces[1][i])
-        for k in range(SUM_AHEAD):
-            if k not in gathered:
-                add_sum1(k)
+        for cols in (scalar_columns((0, first_short)), short_cols):
+            nc.scalar.activation(h_beta[:, 1, cols], h[:, 1, cols], ACT.Identity, bias=beta_columns[:, 1:2])
 
         reciprocal_std(0)
         reciprocal_std(1)

import concourse.mybir as mybir
from concourse.masks import make_identity

F32 = mybir.dt.float32
BF16 = mybir.dt.bfloat16
U16 = mybir.dt.uint16
ALU = mybir.AluOpType
ACT = mybir.ActivationFunctionType
AXIS_X = mybir.AxisListType.X

P = 128
C = 256
CB = C // P
S = 4096
NODES = 17
NICHES = 128
N = NODES * NICHES
LN_EPS = 1e-5
LEAKY_SLOPE = 0.01
TOP_WEIGHT = 99.0
GAMMA_FLOOR = 1e-30

FLOPS = 2 * 2 * C * C * N

PIECE_NODES = ((4, 4, 4, 5), (4, 4, 4, 2, 2, 1))
VECTOR_CHUNKS = ((0, 1), (1, 3), (3, 5), (5, 7), (7, 9))
SCALAR_CHUNKS = ((9, 11), (11, 13), (13, 15), (15, 16), (16, 17))
CHUNKS = VECTOR_CHUNKS + SCALAR_CHUNKS
BANKS = 8
SUM_AHEAD = 5


def node_spans(node_counts):
    spans = []
    first = 0
    for nodes in node_counts:
        spans.append((first, first + nodes))
        first += nodes
    return spans


def tile_gnnnicheencoder_kernel(tc, x, w_l, w_r, b_l, gamma, beta, offs, out):
    nc = tc.nc
    pieces = [node_spans(node_counts) for node_counts in PIECE_NODES]
    chunks = CHUNKS
    n_chunks = len(chunks)
    scalar_nodes = (SCALAR_CHUNKS[0][0], SCALAR_CHUNKS[-1][1])
    with (
        tc.tile_pool(name="held", bufs=1) as held,
        tc.tile_pool(name="work", bufs=n_chunks) as work,
        tc.psum_pool(name="psum", bufs=1) as psum,
    ):
        offsets = held.tile([P, N // 16], U16, name="offsets")
        nc.sync.dma_start(offsets[:], offs)
        store = [held.tile([P, S], F32, name=f"store{cb}") for cb in range(CB)]
        for cb in range(CB):
            for quarter in range(4):
                cells = slice(quarter * S // 4, (quarter + 1) * S // 4)
                nc.sync.dma_start(store[cb][:, cells], x[cb * P : (cb + 1) * P, cells])
        vector_rows = {}
        for name, vec in (("gamma", gamma), ("b_l", b_l), ("beta", beta)):
            vector_rows[name] = held.tile([1, C], F32, name=f"{name}_row")
            nc.scalar.dma_start(vector_rows[name][:], vec.rearrange("c o -> o c"))
        wl_raw = held.tile([P, CB, C], BF16, name="wl_raw")
        wr_raw = held.tile([P, CB, C], BF16, name="wr_raw")
        nc.scalar.dma_start(wl_raw[:], w_l.rearrange("(kb p) c -> p kb c", p=P))
        nc.scalar.dma_start(wr_raw[:], w_r.rearrange("(kb p) c -> p kb c", p=P))

        eps = held.tile([P, 1], F32, name="eps")
        nc.vector.memset(eps[:], LN_EPS)
        identity = held.tile([P, P], F32, name="identity")
        make_identity(nc, identity[:])
        identity_bf = held.tile([P, P], BF16, name="identity_bf")
        nc.vector.tensor_copy(identity_bf[:], identity[:])
        identity_99 = held.tile([P, P], BF16, name="identity_99")
        nc.vector.tensor_scalar_mul(identity_99[:], identity[:], TOP_WEIGHT)
        ones = held.tile([1, P], F32, name="ones")
        nc.vector.memset(ones[:], 1.0)
        ones_bf = held.tile([1, P], BF16, name="ones_bf")
        nc.vector.memset(ones_bf[:], 1.0)
        warm = held.tile([P, 1], F32, name="warm")
        nc.scalar.activation(warm[:], eps[:], ACT.Abs_reciprocal_sqrt)

        sign_row = held.tile([1, C], BF16, name="sign_row")
        nc.vector.tensor_scalar(sign_row[:], vector_rows["gamma"][:], 0.0, 2.0, op0=ALU.is_ge, op1=ALU.mult)
        nc.vector.tensor_scalar_add(sign_row[:], sign_row[:], -1.0)
        sign_spread = psum.tile([P, C], F32, name="sign_spread", tag="bank4")
        nc.tensor.matmul(sign_spread[:], ones_bf[:], sign_row[:], start=True, stop=True)
        sign_rows = held.tile([P, C], F32, name="sign_rows")
        nc.vector.tensor_copy(sign_rows[:], sign_spread[:])
        neg_bias_mean = held.tile([1, 1], F32, name="neg_bias_mean")
        nc.vector.tensor_reduce(neg_bias_mean[:], vector_rows["b_l"][:], axis=AXIS_X, op=ALU.add)
        nc.vector.tensor_scalar_mul(neg_bias_mean[:], neg_bias_mean[:], -1.0 / C)
        bias_bf = held.tile([1, C], BF16, name="bias_bf")
        nc.vector.scalar_tensor_tensor(
            bias_bf[:], vector_rows["b_l"][:], neg_bias_mean[:], sign_row[:], op0=ALU.add, op1=ALU.mult
        )

        neg_mean = {}
        for raw, side in ((wl_raw, "l"), (wr_raw, "r")):
            neg_mean[side] = held.tile([P, CB], F32, name=f"neg_mean_{side}")
            nc.vector.tensor_reduce(neg_mean[side][:], raw[:], axis=AXIS_X, op=ALU.add)
            nc.vector.tensor_scalar_mul(neg_mean[side][:], neg_mean[side][:], -1.0 / C)
        wl_signed = held.tile([P, CB, C], F32, name="wl_signed")
        wr_signed = held.tile([P, CB, C], F32, name="wr_signed")
        w_sum = held.tile([P, CB, C], BF16, name="w_sum")
        w_own = held.tile([P, CB, C], BF16, name="w_own")
        for kb in range(CB):
            for raw, side, signed in ((wl_raw, "l", wl_signed), (wr_raw, "r", wr_signed)):
                nc.vector.scalar_tensor_tensor(
                    signed[:, kb, :], raw[:, kb, :], neg_mean[side][:, kb : kb + 1], sign_rows[:],
                    op0=ALU.add, op1=ALU.mult,
                )
            nc.vector.scalar_tensor_tensor(
                w_own[:, kb, :], wl_signed[:, kb, :], -1.0 / (NODES - 1), wr_signed[:, kb, :],
                op0=ALU.mult, op1=ALU.add,
            )
            nc.vector.tensor_scalar_mul(w_sum[:, kb, :], wl_signed[:, kb, :], 1.0 / (NODES - 1))

        turned_columns = psum.tile([P, 2, CB], F32, name="turned_columns", tag="bank5")
        for v, name in enumerate(("gamma", "beta")):
            for cb in range(CB):
                nc.tensor.matmul(
                    turned_columns[:, v, cb : cb + 1],
                    vector_rows[name][:, cb * P : (cb + 1) * P],
                    ones[:, 0:1],
                    start=True,
                    stop=True,
                )
        columns = held.tile([P, 2, CB], F32, name="columns")
        nc.vector.tensor_copy(columns[:], turned_columns[:])
        gamma_columns, beta_columns = columns[:, 0, :], columns[:, 1, :]
        gamma_abs = held.tile([P, CB], F32, name="gamma_abs")
        nc.vector.scalar_tensor_tensor(gamma_abs[:], gamma_columns, -1.0, gamma_columns, op0=ALU.mult, op1=ALU.max)
        nc.vector.tensor_scalar_max(gamma_abs[:], gamma_abs[:], GAMMA_FLOOR)
        out_scale = held.tile([P, CB], F32, name="out_scale")
        nc.vector.tensor_scalar_mul(out_scale[:], gamma_abs[:], LEAKY_SLOPE)
        shift_columns = held.tile([P, CB], F32, name="shift_columns")
        nc.vector.reciprocal(shift_columns[:], gamma_abs[:])
        nc.vector.tensor_mul(shift_columns[:], shift_columns[:], beta_columns)
        shift_spread = psum.tile([P, C], F32, name="shift_spread", tag="bank6")
        for cb in range(CB):
            nc.tensor.matmul(
                shift_spread[:, cb * P : (cb + 1) * P],
                shift_columns[:, cb : cb + 1].to_broadcast([P, P]),
                identity[:],
                start=True,
                stop=True,
            )
        shift_rows = held.tile([P, C], F32, name="shift_rows")
        nc.vector.tensor_copy(shift_rows[:], shift_spread[:])
        floor_rows = held.tile([P, 2, C], BF16, name="floor_rows")
        nc.vector.tensor_scalar_mul(floor_rows[:], shift_spread[:].unsqueeze(1).to_broadcast([P, 2, C]), -1.0)

        h = held.tile([P, CB, N], F32, name="h")
        h_bf = held.tile([P, CB, N], BF16, name="h_bf")
        h_beta = held.tile([P, CB, N], F32, name="h_beta")
        h_sum = held.tile([P, NICHES], F32, name="h_sum")
        h_sum_bf = held.tile([P, NICHES], BF16, name="h_sum_bf")
        square_sums = held.tile([P, NODES], F32, name="square_sums")
        rstd = held.tile([P, NODES], F32, name="rstd")

        def node_of(tile, kb, node):
            return tile[:, kb, node * NICHES : (node + 1) * NICHES]

        def chunk_of(tile, k):
            first, end = chunks[k]
            return tile[:, :, first * NICHES : end * NICHES].rearrange("p cb (n q) -> p cb n q", q=NICHES)

        def columns_of(kb, i):
            first, end = pieces[kb][i]
            return slice(first * NICHES, end * NICHES)

        def look_up(kb, i):
            cols = columns_of(kb, i)
            nc.scalar.activation(
                h[:, kb, cols], store[kb][:].indirect(offsets[:, cols.start // 16 : cols.stop // 16]), ACT.Copy
            )

        def round_h(kb, i):
            cols = columns_of(kb, i)
            nc.vector.tensor_copy(h_bf[:, kb, cols], h[:, kb, cols])

        def scalar_columns(span):
            return slice(max(span[0], scalar_nodes[0]) * NICHES, min(span[1], scalar_nodes[1]) * NICHES)

        def add_beta(kb, span):
            cols = scalar_columns(span)
            if cols.start < cols.stop:
                nc.vector.tensor_scalar_add(h_beta[:, kb, cols], h[:, kb, cols], beta_columns[:, kb : kb + 1])

        piece_sums = {}

        def halve(i):
            nodes = piece_sums.get(i, h[:, 1, columns_of(1, i)])
            width = nodes.shape[-1] // 2
            half = work.tile([P, width], F32, name=f"half_{width}")
            nc.vector.tensor_add(half[:], nodes[:, :width], nodes[:, width:])
            piece_sums[i] = half[:]

        def add_to_h_sum(i):
            if i == 1:
                return
            so_far = piece_sums[1] if i == 2 else h_sum[:]
            nc.vector.tensor_add(h_sum[:], so_far, piece_sums[i])

        def close_h_sum():
            last = len(pieces[1]) - 1
            last_two = work.tile([P, NICHES], F32, name="last_two")
            nc.vector.tensor_add(last_two[:], piece_sums[last - 1], h[:, 1, columns_of(1, last)])
            nc.vector.tensor_add(h_sum_bf[:], h_sum[:], last_two[:])

        def add_to_sum0(kb, i):
            if kb == 0 and i == 0:
                nc.tensor.matmul(sum0[:], ones_bf[:], bias_bf[:], start=True, stop=False)
            for node in range(*pieces[kb][i]):
                closes = kb == 1 and node == pieces[1][0][1] - 1
                nc.tensor.matmul(sum0[:], node_of(h_bf, kb, node), w_sum[:, kb, :], start=False, stop=closes)

        SUM_BANK = f"bank{BANKS - 1}"
        sum0 = psum.tile([P, C], F32, name="sum0", tag=SUM_BANK)
        sum0_bf = held.tile([P, C], BF16, name="sum0_bf")
        z_banks = {}
        scaled = {}
        turned_banks = {}

        def add_own(k, kb, nodes):
            first, end = chunks[k]
            if kb == 0 and nodes[0] <= first < nodes[1]:
                z_banks[k] = psum.tile([P, end - first, C], F32, name="z_bank", tag=f"bank{k % BANKS}")
            for node in range(max(first, nodes[0]), min(end, nodes[1])):
                nc.tensor.matmul(
                    z_banks[k][:, node - first, :],
                    node_of(h_bf, kb, node),
                    w_own[:, kb, :],
                    start=(kb == 0 and node == first),
                    stop=False,
                )

        def add_sum0(k):
            first, end = chunks[k]
            nc.tensor.matmul(
                z_banks[k][:],
                identity_bf[:],
                sum0_bf[:].unsqueeze(1).to_broadcast([P, end - first, C]),
                start=False,
                stop=False,
            )

        def add_sum1(k):
            first, end = chunks[k]
            nc.tensor.matmul(
                z_banks[k][:],
                h_sum_bf[:],
                w_sum[:, 1, :].unsqueeze(1).to_broadcast([P, end - first, C]),
                start=False,
                stop=True,
            )

        def reciprocal_std(k):
            first, end = chunks[k]
            for node in range(first, end):
                squares = work.tile([P, C], BF16, name="squares")
                nc.scalar.activation(
                    squares[:], z_banks[k][:, node - first, :], ACT.Square, accum_out=square_sums[:, node : node + 1]
                )
            nc.scalar.activation(
                rstd[:, first:end], square_sums[:, first:end], ACT.Abs_reciprocal_sqrt, bias=eps[:, 0:1], scale=1.0 / C
            )

        def by_scalar(k):
            return k >= len(VECTOR_CHUNKS)

        def scale(k):
            first, end = chunks[k]
            scaled[k] = work.tile([P, end - first, C], BF16, name="scaled")
            for node in range(first, end):
                to, z, factor = scaled[k][:, node - first, :], z_banks[k][:, node - first, :], rstd[:, node : node + 1]
                if by_scalar(k):
                    nc.scalar.activation(to, z, ACT.Copy, scale=factor)
                else:
                    nc.vector.scalar_tensor_tensor(to, z, factor, shift_rows[:], op0=ALU.mult, op1=ALU.add)

        def turn_back(k):
            first, end = chunks[k]
            top = work.tile([P, end - first, C], BF16, name="top")
            if by_scalar(k):
                nc.vector.tensor_tensor(top[:], scaled[k][:], floor_rows[:, : end - first, :], ALU.max)
            else:
                nc.vector.tensor_scalar_max(top[:], scaled[k][:], 0.0)
            turned_banks[k] = psum.tile([P, CB, end - first, NICHES], F32, name="turned_bank", tag=f"bank{k % BANKS}")
            terms = [
                (part, eye, node, cb)
                for part, eye in ((scaled[k], identity_bf), (top, identity_99))
                for node in range(end - first)
                for cb in range(CB)
            ]
            for t, (part, eye, node, cb) in enumerate(terms):
                nc.tensor.matmul(
                    turned_banks[k][:, cb, node, :],
                    part[:, node, cb * P : (cb + 1) * P],
                    eye[:],
                    start=(t == 0),
                    stop=(t == len(terms) - 1),
                )

        def finish(k):
            first, end = chunks[k]
            residual = chunk_of(h_beta if by_scalar(k) else h, k)
            result = work.tile([P, CB, end - first, NICHES], F32, name="result")
            for cb in range(CB):
                nc.vector.scalar_tensor_tensor(
                    result[:, cb], turned_banks[k][:, cb], out_scale[:, cb : cb + 1], residual[:, cb],
                    op0=ALU.mult, op1=ALU.add,
                )
            nc.sync.dma_start(
                out.rearrange("(cb p) j -> p cb j", p=P)[:, :, first * NICHES : end * NICHES],
                result[:].rearrange("p cb n q -> p cb (n q)"),
            )

        early = range(BANKS - 1)
        for i, span in enumerate(pieces[0]):
            look_up(0, i)
            round_h(0, i)
            add_to_sum0(0, i)
            for k in early:
                add_own(k, 0, span)
            add_beta(0, span)
        short = [i for i, (first, end) in enumerate(pieces[1]) if end - first < 4]
        for i in range(short[0]):
            look_up(1, i)
            if i > 0:
                halve(i)
            if i > 1:
                add_to_h_sum(i - 1)
            round_h(1, i)
            if i > 0:
                halve(i)
            for k in early:
                add_own(k, 1, pieces[1][i])
            if i == 0:
                add_to_sum0(1, i)
            if i == 1:
                nc.vector.tensor_copy(sum0_bf[:], sum0[:])
        for k in early:
            add_sum0(k)
        for i in short:
            look_up(1, i)
            if i != short[-1]:
                halve(i)
                add_to_h_sum(i - 1)
        close_h_sum()
        for k in range(SUM_AHEAD):
            add_sum1(k)
        first_short = pieces[1][short[0]][0]
        short_cols = slice(first_short * NICHES, N)
        nc.scalar.copy(h_bf[:, 1, short_cols], h[:, 1, short_cols])
        for i in short:
            for k in early:
                add_own(k, 1, pieces[1][i])
        for cols in (scalar_columns((0, first_short)), short_cols):
            nc.scalar.activation(h_beta[:, 1, cols], h[:, 1, cols], ACT.Identity, bias=beta_columns[:, 1:2])

        reciprocal_std(0)
        reciprocal_std(1)
        scale(0)
        for step in range(n_chunks + 2):
            if step + 2 < n_chunks:
                reciprocal_std(step + 2)
            if step + 1 < n_chunks:
                scale(step + 1)
            if step < n_chunks:
                turn_back(step)
            if step >= 2:
                finish(step - 2)
            if step + SUM_AHEAD < BANKS - 1:
                add_sum1(step + SUM_AHEAD)
            for k in range(BANKS - 1, n_chunks):
                if step == max(0, k - BANKS + 2):
                    for kb in range(CB):
                        add_own(k, kb, chunks[k])
                    add_sum0(k)
                    add_sum1(k)
